import numpy as np
import ml_dtypes


def mxq(x, axis, fmt="e4m3"):
    dtype, down = {"e4m3": (ml_dtypes.float8_e4m3fn, 7), "e5m2": (ml_dtypes.float8_e5m2, 14)}[fmt]
    v = np.moveaxis(np.asarray(x, np.float32).astype(ml_dtypes.bfloat16).astype(np.float64), axis, -1)
    blocks = v.reshape(v.shape[:-1] + (-1, 32))
    amax = np.abs(blocks).max(-1, keepdims=True)
    byte = np.maximum(np.where(amax > 0, np.frexp(amax)[1] - 1 + 127, 0) - down, 1)
    scale = np.exp2(byte - 127.0)
    codes = (blocks / scale).astype(np.float32).astype(dtype).astype(np.float64)
    return np.moveaxis((codes * scale).reshape(v.shape), -1, axis)


WIDE = False


def mx_kscale(k):
    if not WIDE:
        return np.ones(k)
    levels = np.array([10, -10, 5, -5, 0])
    a = np.random.permutation(np.resize(levels, k // 512 * 4)).reshape(k // 512, 4)
    idx = np.arange(k)
    return np.exp2(a[idx // 512, idx % 128 // 32])


BF16 = ml_dtypes.bfloat16


def bf(x):
    return np.asarray(x, np.float32).astype(BF16)


def f64(x):
    return np.asarray(x).astype(np.float64)


E2M1 = np.array([0.0, 0.5, 1.0, 1.5, 2.0, 3.0, 4.0, 6.0, -0.0, -0.5, -1.0, -1.5, -2.0, -3.0, -4.0, -6.0])


def pack_weight(w, fmt):
    k, n = w.shape
    w = f64(bf(w)).reshape(k // 32, 32, n)
    amax = np.abs(w).max(1)
    if fmt == "e4m3":
        byte = np.frexp(amax)[1] - 1 + 127 - 7
    else:
        mant, ex = np.frexp(amax / 6.0)
        byte = np.where(mant > 0.5, ex, ex - 1) + 127
    byte = np.clip(np.where(amax > 0, byte, 1), 1, 254)
    scaled = (w * np.exp2(127.0 - byte)[:, None, :]).reshape(k, n).astype(np.float32)
    by_word = np.ascontiguousarray(scaled.reshape(k // 512, 128, 4, n).transpose(0, 1, 3, 2))
    if fmt == "e4m3":
        words = by_word.astype(ml_dtypes.float8_e4m3fn).view(np.uint8)
    else:
        c = by_word.astype(ml_dtypes.float4_e2m1fn).view(np.uint8) & 0xF
        words = c[..., 0::2] | (c[..., 1::2] << 4)
    return np.ascontiguousarray(words), np.ascontiguousarray(byte.astype(np.uint8).reshape(k // 512, 16, n))


def unpack_weight(words, scales, fmt):
    g, p, n, _ = words.shape
    if fmt == "e4m3":
        vals = np.ascontiguousarray(words).view(ml_dtypes.float8_e4m3fn).astype(np.float64)
    else:
        nib = np.empty((g, p, n, 4), np.uint8)
        nib[..., 0::2] = words & 0xF
        nib[..., 1::2] = words >> 4
        vals = E2M1[nib]
    vals = vals * np.repeat(np.exp2(scales.astype(np.float64) - 127.0), 8, axis=1)[..., None]
    return vals.transpose(0, 1, 3, 2).reshape(g * 512, n)

def pack4(w):
    words, scales = pack_weight(w, "e2m1")
    return words.reshape(words.shape[0], 128, -1), scales


def unpack4(words, scales):
    return unpack_weight(words.reshape(words.shape[0], 128, -1, 2), scales, "e2m1")


C, I, T, R, D = 8, 8, 128, 512, 256


def sigmoid(v):
    return 1.0 / (1.0 + np.exp(-v))


def setup_inputs():
    s = mx_kscale(D + D)[D:]
    u = np.concatenate([np.ones(D), s])[:, None]
    query = bf(np.random.standard_normal((C, I, T, D)) * 0.5)
    wc = bf(np.random.standard_normal((C, I, T, D)) * 6.0 / np.sqrt(R) * s)
    w_lin_words, w_lin_scales = pack4(np.random.standard_normal((D + D, D)) * 1.5 / np.sqrt(D) / u)
    b_lin = bf(np.random.standard_normal(D) * 0.2)
    w_gate_words, w_gate_scales = pack4(np.random.standard_normal((D + D, D)) * 1.5 / np.sqrt(D) / u)
    b_gate = bf(np.random.standard_normal(D) * 0.2)
    return {"query": query,
            "wc": wc,
            "w_lin_words": w_lin_words,
            "w_lin_scales": w_lin_scales,
            "b_lin": b_lin,
            "w_gate_words": w_gate_words,
            "w_gate_scales": w_gate_scales,
            "b_gate": b_gate}


def reference(query, wc, w_lin_words, w_lin_scales, b_lin, w_gate_words, w_gate_scales, b_gate):
    q = f64(query)
    cat = mxq(np.concatenate([q, f64(wc)], axis=-1), 3, "e4m3")
    upd = np.tanh((cat @ unpack4(w_lin_words, w_lin_scales)) + f64(b_lin))
    gate = sigmoid((cat @ unpack4(w_gate_words, w_gate_scales)) + f64(b_gate))
    return q * gate + upd * (1.0 - gate)

@@ -1,0 +1,194 @@
+from contextlib import ExitStack
+
+import concourse.mybir as mybir
+from concourse.masks import make_identity
+
+F32 = mybir.dt.float32
+BF16 = mybir.dt.bfloat16
+I32 = mybir.dt.int32
+U32 = mybir.dt.uint32
+U8 = mybir.dt.uint8
+FP8X4 = mybir.dt.float8_e4m3fn_x4
+FP4X4 = mybir.dt.float4_e2m1fn_x4
+ACT = mybir.ActivationFunctionType
+ALU = mybir.AluOpType
+
+P = 128
+D = 256
+K = 2 * D
+TOKENS = 8 * 8 * 128
+TILES = 4
+ROUND = TILES * P
+ROUNDS = TOKENS // ROUND
+HALVES = 2
+BLOCKS = 4
+LOAD_AHEAD = 5
+
+FLOPS = 2 * TOKENS * K * (2 * D)
+
+
+def tile_scan_pb_t_kernel(
+    tc, query, wc, w_lin_words, w_lin_scales, b_lin, w_gate_words, w_gate_scales, b_gate, out
+):
+    nc = tc.nc
+
+    q_rounds = query.flatten_outer_dims().rearrange("(r p j) d -> r p j d", p=P, j=TILES)
+    wc_rounds = wc.flatten_outer_dims().rearrange("(r p j) d -> r p j d", p=P, j=TILES)
+    out_rounds = out.flatten_outer_dims().rearrange("(r p j) d -> r p j d", p=P, j=TILES)
+
+    with ExitStack() as stack:
+        const = stack.enter_context(tc.tile_pool(name="const", bufs=1))
+        cat_pool = stack.enter_context(tc.tile_pool(name="cat", bufs=ROUNDS))
+        mx_pool = stack.enter_context(tc.tile_pool(name="mx", bufs=2))
+        act_pool = stack.enter_context(tc.tile_pool(name="act", bufs=2))
+        blend_pool = stack.enter_context(tc.tile_pool(name="blend", bufs=4))
+        psum = stack.enter_context(tc.psum_pool(name="psum", bufs=1))
+        stack.enter_context(tc.manual_schedule())
+
+        cat = {}
+        cat_t = {}
+        grouped = {}
+        codes = {}
+        product = {}
+        activated = {}
+
+        def load(r):
+            cat[r] = cat_pool.tile([P, TILES, K], BF16, name="cat")
+            nc.sync.dma_start(out=cat[r][:, :, 0:D], in_=q_rounds[r])
+            nc.sync.dma_start(out=cat[r][:, :, D:K], in_=wc_rounds[r])
+
+        def transpose_cat(r):
+            cat_t[r] = []
+            for bank in range(HALVES):
+                words_t = psum.tile([P, 2, 2, P], F32, name="words_t", tag="cat_t%d" % bank)
+                for jj in range(2):
+                    words = cat[r][:, 2 * bank + jj, :].bitcast(F32)
+                    for u in range(2):
+                        nc.tensor.transpose(words_t[:, jj, u, :], words[:, u : K // 2 : 2], ident[:])
+                cat_t[r].append(words_t)
+
+        def regroup(r):
+            grouped[r] = mx_pool.tile([P, TILES, P, 4], BF16, name="grouped", align_bytes=64)
+            for bank in range(HALVES):
+                nc.scalar.copy(
+                    out=grouped[r][:, 2 * bank : 2 * bank + 2, :, :].bitcast(F32),
+                    in_=cat_t[r][bank][:].rearrange("p j u t -> p j t u"),
+                )
+
+        def quantise(r):
+            words = mx_pool.tile([P, ROUND], U32, name="code_words", align_bytes=64)
+            scales = mx_pool.tile([P, ROUND], U8, name="code_scales", align_bytes=64)
+            nc.vector.quantize_mx(
+                out=words[:].bitcast(FP8X4),
+                scales=scales[:],
+                in_=grouped[r][:].rearrange("p j t k -> p (j t k)"),
+            )
+            codes[r] = (words, scales)
+
+        def multiply(r):
+            words, scales = codes[r]
+            product[r] = []
+            for b in range(BLOCKS):
+                acc = psum.tile([P, ROUND], F32, name="acc", tag="product%d" % b)
+                nc.tensor.matmul_mx(
+                    out=acc[:],
+                    lhsT=w_words[:, 2 * P * b : 2 * P * (b + 1)].bitcast(FP4X4),
+                    lhsT_scale=w_scales[:, P * b : P * (b + 1)],
+                    rhs=words[:].bitcast(FP8X4),
+                    rhs_scale=scales[:],
+                    start=True,
+                    stop=True,
+                )
+                product[r].append(acc)
+
+        def activate(r):
+            activated[r] = []
+            for b in range(BLOCKS):
+                is_gate = b >= BLOCKS // 2
+                act = act_pool.tile([P, ROUND], F32, name="act", tag="act%d" % b)
+                nc.scalar.activation(
+                    out=act[:],
+                    in_=product[r][b][:],
+                    func=ACT.Sigmoid if is_gate else ACT.Tanh,
+                    bias=bias_col[:, b : b + 1],
+                    scale=-1.0 if is_gate else 1.0,
+                )
+                activated[r].append(act)
+
+        def transpose_back(r, half):
+            banks = []
+            for kind, tag in enumerate(("upd", "keep")):
+                bank = psum.tile([P, 2, D], F32, name="bank", tag=tag)
+                for jj in range(2):
+                    tokens = slice(P * (2 * half + jj), P * (2 * half + jj + 1))
+                    for c in range(2):
+                        nc.tensor.transpose(
+                            bank[:, jj, P * c : P * (c + 1)], activated[r][2 * kind + c][:, tokens], ident[:]
+                        )
+                banks.append(bank)
+            return banks
+
+        def blend(r, half, upd, keep):
+            tiles = slice(2 * half, 2 * half + 2)
+            q = cat[r][:, tiles, 0:D]
+            diff = blend_pool.tile([P, 2, D], F32, name="diff")
+            nc.vector.tensor_tensor(out=diff[:], in0=upd[:], in1=q, op=ALU.subtract)
+            step = blend_pool.tile([P, 2, D], F32, name="step")
+            nc.vector.tensor_tensor(out=step[:], in0=keep[:], in1=diff[:], op=ALU.mult)
+            result = blend_pool.tile([P, 2, D], F32, name="result")
+            nc.gpsimd.tensor_tensor(out=result[:], in0=step[:], in1=q, op=ALU.add)
+            nc.sync.dma_start(out=out_rounds[r][:, tiles, :], in_=result[:])
+
+        ident = const.tile([P, P], F32, name="ident")
+        make_identity(nc, ident[:])
+
+        w_scales = const.tile([P, BLOCKS * P], U8, name="w_scales", align_bytes=64)
+        nc.vector.memset(w_scales[:].bitcast(I32), 0)
+        w_words = const.tile([P, BLOCKS * 2 * P], U8, name="w_words", align_bytes=64)
+        bias_rows = const.tile([P, P], BF16, name="bias_rows")
+        nc.vector.memset(bias_rows[:], 0.0)
+
+        load(0)
+        weights = ((w_lin_words, w_lin_scales, b_lin), (w_gate_words, w_gate_scales, b_gate))
+        for i, (dram_words, dram_scales, dram_bias) in enumerate(weights):
+            nc.scalar.dma_start(out=bias_rows[2 * i : 2 * i + 2, :], in_=dram_bias.rearrange("(r c) -> r c", c=P))
+            nc.sync.dma_start(
+                out=w_words[:, 2 * D * i : 2 * D * (i + 1)].bitcast(I32), in_=dram_words[0].bitcast(I32)
+            )
+            for quad in range(4):
+                nc.sync.dma_start(
+                    out=w_scales[32 * quad : 32 * quad + 4, D * i : D * (i + 1)].bitcast(I32),
+                    in_=dram_scales[0, 4 * quad : 4 * quad + 4, :].bitcast(I32),
+                )
+        for r in range(1, LOAD_AHEAD):
+            load(r)
+
+        bias_f32 = const.tile([P, P], F32, name="bias_f32")
+        nc.vector.tensor_copy(out=bias_f32[:], in_=bias_rows[:])
+        bias_t = psum.tile([P, P], F32, name="bias_t", tag="upd")
+        nc.tensor.transpose(bias_t[:], bias_f32[:], ident[:])
+        bias_col = const.tile([P, BLOCKS], F32, name="bias_col")
+        nc.vector.tensor_copy(out=bias_col[:, 0:2], in_=bias_t[:, 0:2])
+        nc.vector.tensor_scalar_mul(out=bias_col[:, 2:4], in0=bias_t[:, 2:4], scalar1=-1.0)
+
+        def live(r):
+            return 0 <= r < ROUNDS
+
+        for s in range(-1, ROUNDS + 2):
+            if s + 1 + LOAD_AHEAD < ROUNDS:
+                load(s + 1 + LOAD_AHEAD)
+            if live(s):
+                quantise(s)
+            if live(s - 1):
+                activate(s - 1)
+            if live(s - 2):
+                upd, keep = transpose_back(s - 2, 0)
+                blend(s - 2, 0, upd, keep)
+            if live(s + 1):
+                transpose_cat(s + 1)
+                regroup(s + 1)
+            if live(s - 2):
+                upd, keep = transpose_back(s - 2, 1)
+                blend(s - 2, 1, upd, keep)
+            if live(s):
+                multiply(s)

@@ -22,7 +22,9 @@ ROUND = TILES * P
 ROUNDS = TOKENS // ROUND
 HALVES = 2
 BLOCKS = 4
-LOAD_AHEAD = 5
+LIN_BLOCKS = (0, 1)
+GATE_BLOCKS = (2, 3)
+LOAD_AHEAD = 4
 
 FLOPS = 2 * TOKENS * K * (2 * D)
 
@@ -46,7 +48,6 @@ def tile_scan_pb_t_kernel(
         stack.enter_context(tc.manual_schedule())
 
         cat = {}
-        cat_t = {}
         grouped = {}
         codes = {}
         product = {}
@@ -57,23 +58,21 @@ def tile_scan_pb_t_kernel(
             nc.sync.dma_start(out=cat[r][:, :, 0:D], in_=q_rounds[r])
             nc.sync.dma_start(out=cat[r][:, :, D:K], in_=wc_rounds[r])
 
-        def transpose_cat(r):
-            cat_t[r] = []
-            for bank in range(HALVES):
-                words_t = psum.tile([P, 2, 2, P], F32, name="words_t", tag="cat_t%d" % bank)
-                for jj in range(2):
-                    words = cat[r][:, 2 * bank + jj, :].bitcast(F32)
-                    for u in range(2):
-                        nc.tensor.transpose(words_t[:, jj, u, :], words[:, u : K // 2 : 2], ident[:])
-                cat_t[r].append(words_t)
+        def transpose_cat(r, half):
+            words_t = psum.tile([P, 2, 2, P], F32, name="words_t", tag="cat_t%d" % half)
+            for jj in range(2):
+                words = cat[r][:, 2 * half + jj, :].bitcast(F32)
+                for u in range(2):
+                    nc.tensor.transpose(words_t[:, jj, u, :], words[:, u : K // 2 : 2], ident[:])
+            return words_t
 
-        def regroup(r):
-            grouped[r] = mx_pool.tile([P, TILES, P, 4], BF16, name="grouped", align_bytes=64)
-            for bank in range(HALVES):
-                nc.scalar.copy(
-                    out=grouped[r][:, 2 * bank : 2 * bank + 2, :, :].bitcast(F32),
-                    in_=cat_t[r][bank][:].rearrange("p j u t -> p j t u"),
-                )
+        def regroup(r, half, words_t):
+            if half == 0:
+                grouped[r] = mx_pool.tile([P, TILES, P, 4], BF16, name="grouped", align_bytes=64)
+            nc.scalar.copy(
+                out=grouped[r][:, 2 * half : 2 * half + 2, :, :].bitcast(F32),
+                in_=words_t[:].rearrange("p j u t -> p j t u"),
+            )
 
         def quantise(r):
             words = mx_pool.tile([P, ROUND], U32, name="code_words", align_bytes=64)
@@ -85,10 +84,9 @@ def tile_scan_pb_t_kernel(
             )
             codes[r] = (words, scales)
 
-        def multiply(r):
+        def multiply(r, blocks):
             words, scales = codes[r]
-            product[r] = []
-            for b in range(BLOCKS):
+            for b in blocks:
                 acc = psum.tile([P, ROUND], F32, name="acc", tag="product%d" % b)
                 nc.tensor.matmul_mx(
                     out=acc[:],
@@ -99,21 +97,20 @@ def tile_scan_pb_t_kernel(
                     start=True,
                     stop=True,
                 )
-                product[r].append(acc)
+                product[r, b] = acc
 
-        def activate(r):
-            activated[r] = []
-            for b in range(BLOCKS):
-                is_gate = b >= BLOCKS // 2
+        def activate(r, blocks):
+            for b in blocks:
+                is_gate = b in GATE_BLOCKS
                 act = act_pool.tile([P, ROUND], F32, name="act", tag="act%d" % b)
                 nc.scalar.activation(
                     out=act[:],
-                    in_=product[r][b][:],
+                    in_=product[r, b][:],
                     func=ACT.Sigmoid if is_gate else ACT.Tanh,
                     bias=bias_col[:, b : b + 1],
                     scale=-1.0 if is_gate else 1.0,
                 )
-                activated[r].append(act)
+                activated[r, b] = act
 
         def transpose_back(r, half):
             banks = []
@@ -123,7 +120,7 @@ def tile_scan_pb_t_kernel(
                     tokens = slice(P * (2 * half + jj), P * (2 * half + jj + 1))
                     for c in range(2):
                         nc.tensor.transpose(
-                            bank[:, jj, P * c : P * (c + 1)], activated[r][2 * kind + c][:, tokens], ident[:]
+                            bank[:, jj, P * c : P * (c + 1)], activated[r, 2 * kind + c][:, tokens], ident[:]
                         )
                 banks.append(bank)
             return banks
@@ -174,21 +171,28 @@ def tile_scan_pb_t_kernel(
         def live(r):
             return 0 <= r < ROUNDS
 
-        for s in range(-1, ROUNDS + 2):
-            if s + 1 + LOAD_AHEAD < ROUNDS:
-                load(s + 1 + LOAD_AHEAD)
+        def prepare(r, half):
+            if live(r):
+                words_t = transpose_cat(r, half)
+                regroup(r, half, words_t)
+
+        def finish(r, half):
+            if live(r):
+                upd, keep = transpose_back(r, half)
+                blend(r, half, upd, keep)
+
+        for s in range(-2, ROUNDS + 1):
+            if s + 2 + LOAD_AHEAD < ROUNDS:
+                load(s + 2 + LOAD_AHEAD)
             if live(s):
-                quantise(s)
-            if live(s - 1):
-                activate(s - 1)
-            if live(s - 2):
-                upd, keep = transpose_back(s - 2, 0)
-                blend(s - 2, 0, upd, keep)
+                multiply(s, LIN_BLOCKS)
+                activate(s, LIN_BLOCKS)
+            prepare(s + 1, 1)
+            finish(s - 1, 0)
             if live(s + 1):
-                transpose_cat(s + 1)
-                regroup(s + 1)
-            if live(s - 2):
-                upd, keep = transpose_back(s - 2, 1)
-                blend(s - 2, 1, upd, keep)
+                quantise(s + 1)
             if live(s):
-                multiply(s)
+                multiply(s, GATE_BLOCKS)
+                activate(s, GATE_BLOCKS)
+            prepare(s + 2, 0)
+            finish(s - 1, 1)

@@ -20,11 +20,14 @@ TOKENS = 8 * 8 * 128
 TILES = 4
 ROUND = TILES * P
 ROUNDS = TOKENS // ROUND
-HALVES = 2
+HALF = ROUND // 2
+HALF_ROUNDS = 2 * ROUNDS
 BLOCKS = 4
 LIN_BLOCKS = (0, 1)
 GATE_BLOCKS = (2, 3)
 LOAD_AHEAD = 4
+CAT_LEAD = 4
+BACK_LAG = 2
 
 FLOPS = 2 * TOKENS * K * (2 * D)
 
@@ -41,10 +44,12 @@ def tile_scan_pb_t_kernel(
     with ExitStack() as stack:
         const = stack.enter_context(tc.tile_pool(name="const", bufs=1))
         cat_pool = stack.enter_context(tc.tile_pool(name="cat", bufs=ROUNDS))
-        mx_pool = stack.enter_context(tc.tile_pool(name="mx", bufs=2))
+        mx_pool = stack.enter_context(tc.tile_pool(name="mx", bufs=3))
         act_pool = stack.enter_context(tc.tile_pool(name="act", bufs=2))
         blend_pool = stack.enter_context(tc.tile_pool(name="blend", bufs=4))
-        psum = stack.enter_context(tc.psum_pool(name="psum", bufs=1))
+        cat_t_psum = stack.enter_context(tc.psum_pool(name="cat_t_psum", bufs=2))
+        product_psum = stack.enter_context(tc.psum_pool(name="product_psum", bufs=3))
+        back_psum = stack.enter_context(tc.psum_pool(name="back_psum", bufs=3))
         stack.enter_context(tc.manual_schedule())
 
         cat = {}
@@ -58,42 +63,43 @@ def tile_scan_pb_t_kernel(
             nc.sync.dma_start(out=cat[r][:, :, 0:D], in_=q_rounds[r])
             nc.sync.dma_start(out=cat[r][:, :, D:K], in_=wc_rounds[r])
 
-        def transpose_cat(r, half):
-            words_t = psum.tile([P, 2, 2, P], F32, name="words_t", tag="cat_t%d" % half)
+        def transpose_cat(c):
+            r, half = divmod(c, 2)
+            words_t = cat_t_psum.tile([P, 2, 2, P], F32, name="words_t")
             for jj in range(2):
                 words = cat[r][:, 2 * half + jj, :].bitcast(F32)
                 for u in range(2):
                     nc.tensor.transpose(words_t[:, jj, u, :], words[:, u : K // 2 : 2], ident[:])
             return words_t
 
-        def regroup(r, half, words_t):
-            if half == 0:
-                grouped[r] = mx_pool.tile([P, TILES, P, 4], BF16, name="grouped", align_bytes=64)
-            nc.scalar.copy(
-                out=grouped[r][:, 2 * half : 2 * half + 2, :, :].bitcast(F32),
-                in_=words_t[:].rearrange("p j u t -> p j t u"),
-            )
+        def regroup(c, words_t):
+            grouped[c] = mx_pool.tile([P, 2, P, 4], BF16, name="grouped", align_bytes=64)
+            nc.scalar.copy(out=grouped[c][:].bitcast(F32), in_=words_t[:].rearrange("p j u t -> p j t u"))
 
-        def quantise(r):
-            words = mx_pool.tile([P, ROUND], U32, name="code_words", align_bytes=64)
-            scales = mx_pool.tile([P, ROUND], U8, name="code_scales", align_bytes=64)
+        def quantise(c):
+            r, half = divmod(c, 2)
+            if half == 0:
+                code_words = mx_pool.tile([P, ROUND], U32, name="code_words", align_bytes=64)
+                code_scales = mx_pool.tile([P, ROUND], U8, name="code_scales", align_bytes=64)
+                codes[r] = (code_words, code_scales)
+            code_words, code_scales = codes[r]
+            tokens = slice(HALF * half, HALF * (half + 1))
             nc.vector.quantize_mx(
-                out=words[:].bitcast(FP8X4),
-                scales=scales[:],
-                in_=grouped[r][:].rearrange("p j t k -> p (j t k)"),
+                out=code_words[:, tokens].bitcast(FP8X4),
+                scales=code_scales[:, tokens],
+                in_=grouped[c][:].rearrange("p j t k -> p (j t k)"),
             )
-            codes[r] = (words, scales)
 
         def multiply(r, blocks):
-            words, scales = codes[r]
+            code_words, code_scales = codes[r]
             for b in blocks:
-                acc = psum.tile([P, ROUND], F32, name="acc", tag="product%d" % b)
+                acc = product_psum.tile([P, ROUND], F32, name="acc")
                 nc.tensor.matmul_mx(
                     out=acc[:],
                     lhsT=w_words[:, 2 * P * b : 2 * P * (b + 1)].bitcast(FP4X4),
                     lhsT_scale=w_scales[:, P * b : P * (b + 1)],
-                    rhs=words[:].bitcast(FP8X4),
-                    rhs_scale=scales[:],
+                    rhs=code_words[:].bitcast(FP8X4),
+                    rhs_scale=code_scales[:],
                     start=True,
                     stop=True,
                 )
@@ -112,27 +118,29 @@ def tile_scan_pb_t_kernel(
                 )
                 activated[r, b] = act
 
-        def transpose_back(r, half):
+        def transpose_back(c):
+            r, half = divmod(c, 2)
             banks = []
-            for kind, tag in enumerate(("upd", "keep")):
-                bank = psum.tile([P, 2, D], F32, name="bank", tag=tag)
+            for blocks in (LIN_BLOCKS, GATE_BLOCKS):
+                bank = back_psum.tile([P, 2, D], F32, name="bank")
                 for jj in range(2):
                     tokens = slice(P * (2 * half + jj), P * (2 * half + jj + 1))
-                    for c in range(2):
-                        nc.tensor.transpose(
-                            bank[:, jj, P * c : P * (c + 1)], activated[r, 2 * kind + c][:, tokens], ident[:]
-                        )
+                    for i, b in enumerate(blocks):
+                        nc.tensor.transpose(bank[:, jj, P * i : P * (i + 1)], activated[r, b][:, tokens], ident[:])
                 banks.append(bank)
             return banks
 
-        def blend(r, half, upd, keep):
+        def blend(c, upd, keep):
+            r, half = divmod(c, 2)
             tiles = slice(2 * half, 2 * half + 2)
             q = cat[r][:, tiles, 0:D]
             diff = blend_pool.tile([P, 2, D], F32, name="diff")
-            nc.vector.tensor_tensor(out=diff[:], in0=upd[:], in1=q, op=ALU.subtract)
             step = blend_pool.tile([P, 2, D], F32, name="step")
-            nc.vector.tensor_tensor(out=step[:], in0=keep[:], in1=diff[:], op=ALU.mult)
             result = blend_pool.tile([P, 2, D], F32, name="result")
+            for jj in range(2):
+                nc.vector.tensor_tensor(out=diff[:, jj, :], in0=upd[:, jj, :], in1=q[:, jj, :], op=ALU.subtract)
+            for jj in range(2):
+                nc.vector.tensor_tensor(out=step[:, jj, :], in0=keep[:, jj, :], in1=diff[:, jj, :], op=ALU.mult)
             nc.gpsimd.tensor_tensor(out=result[:], in0=step[:], in1=q, op=ALU.add)
             nc.sync.dma_start(out=out_rounds[r][:, tiles, :], in_=result[:])
 
@@ -162,37 +170,28 @@ def tile_scan_pb_t_kernel(
 
         bias_f32 = const.tile([P, P], F32, name="bias_f32")
         nc.vector.tensor_copy(out=bias_f32[:], in_=bias_rows[:])
-        bias_t = psum.tile([P, P], F32, name="bias_t", tag="upd")
+        bias_t = back_psum.tile([P, P], F32, name="bias_t", tag="bank")
         nc.tensor.transpose(bias_t[:], bias_f32[:], ident[:])
         bias_col = const.tile([P, BLOCKS], F32, name="bias_col")
         nc.vector.tensor_copy(out=bias_col[:, 0:2], in_=bias_t[:, 0:2])
         nc.vector.tensor_scalar_mul(out=bias_col[:, 2:4], in0=bias_t[:, 2:4], scalar1=-1.0)
 
-        def live(r):
-            return 0 <= r < ROUNDS
+        def live(c):
+            return 0 <= c < HALF_ROUNDS
 
-        def prepare(r, half):
-            if live(r):
-                words_t = transpose_cat(r, half)
-                regroup(r, half, words_t)
-
-        def finish(r, half):
-            if live(r):
-                upd, keep = transpose_back(r, half)
-                blend(r, half, upd, keep)
-
-        for s in range(-2, ROUNDS + 1):
-            if s + 2 + LOAD_AHEAD < ROUNDS:
-                load(s + 2 + LOAD_AHEAD)
-            if live(s):
-                multiply(s, LIN_BLOCKS)
-                activate(s, LIN_BLOCKS)
-            prepare(s + 1, 1)
-            finish(s - 1, 0)
-            if live(s + 1):
-                quantise(s + 1)
-            if live(s):
-                multiply(s, GATE_BLOCKS)
-                activate(s, GATE_BLOCKS)
-            prepare(s + 2, 0)
-            finish(s - 1, 1)
+        for h in range(-CAT_LEAD, HALF_ROUNDS + BACK_LAG):
+            r, half = divmod(h, 2)
+            if half == 0 and r + CAT_LEAD // 2 + LOAD_AHEAD < ROUNDS:
+                load(r + CAT_LEAD // 2 + LOAD_AHEAD)
+            if live(h):
+                blocks = LIN_BLOCKS if half == 0 else GATE_BLOCKS
+                multiply(r, blocks)
+                activate(r, blocks)
+            if live(h + CAT_LEAD):
+                words_t = transpose_cat(h + CAT_LEAD)
+                regroup(h + CAT_LEAD, words_t)
+            if live(h - BACK_LAG):
+                upd, keep = transpose_back(h - BACK_LAG)
+                blend(h - BACK_LAG, upd, keep)
+            if live(h + CAT_LEAD - 1):
+                quantise(h + CAT_LEAD - 1)

@@ -135,28 +135,42 @@ def tile_scan_pb_t_kernel(
             tiles = slice(2 * half, 2 * half + 2)
             q = cat[r][:, tiles, 0:D]
             diff = blend_pool.tile([P, 2, D], F32, name="diff")
-            step = blend_pool.tile([P, 2, D], F32, name="step")
+            change = blend_pool.tile([P, 2, D], F32, name="change")
             result = blend_pool.tile([P, 2, D], F32, name="result")
             for jj in range(2):
                 nc.vector.tensor_tensor(out=diff[:, jj, :], in0=upd[:, jj, :], in1=q[:, jj, :], op=ALU.subtract)
             for jj in range(2):
-                nc.vector.tensor_tensor(out=step[:, jj, :], in0=keep[:, jj, :], in1=diff[:, jj, :], op=ALU.mult)
-            nc.gpsimd.tensor_tensor(out=result[:], in0=step[:], in1=q, op=ALU.add)
+                nc.vector.tensor_tensor(out=change[:, jj, :], in0=keep[:, jj, :], in1=diff[:, jj, :], op=ALU.mult)
+            if c < HALF_ROUNDS - 1:
+                nc.gpsimd.tensor_tensor(out=result[:], in0=change[:], in1=q, op=ALU.add)
+            else:
+                for jj in range(2):
+                    nc.vector.tensor_tensor(out=result[:, jj, :], in0=change[:, jj, :], in1=q[:, jj, :], op=ALU.add)
             nc.sync.dma_start(out=out_rounds[r][:, tiles, :], in_=result[:])
 
+        def spread_biases():
+            bias_t = back_psum.tile([P, P], F32, name="bias_t", tag="bank")
+            nc.tensor.transpose(bias_t[:], bias_f32[:], ident[:])
+            nc.vector.tensor_copy(out=bias_col[:, 0:2], in_=bias_t[:, 0:2])
+            nc.vector.tensor_scalar_mul(out=bias_col[:, 2:4], in0=bias_t[:, 2:4], scalar1=-1.0)
+
+        bias_rows = const.tile([P, P], BF16, name="bias_rows")
+        bias_col = const.tile([P, BLOCKS], F32, name="bias_col")
+        nc.vector.memset(bias_rows[:], 0.0)
+        nc.gpsimd.dma_start(out=bias_rows[0:2, :], in_=b_lin.rearrange("(r c) -> r c", c=P))
+        nc.gpsimd.dma_start(out=bias_rows[2:4, :], in_=b_gate.rearrange("(r c) -> r c", c=P))
         ident = const.tile([P, P], F32, name="ident")
         make_identity(nc, ident[:])
+        bias_f32 = const.tile([P, P], F32, name="bias_f32")
+        nc.vector.tensor_copy(out=bias_f32[:], in_=bias_rows[:])
 
+        w_words = const.tile([P, BLOCKS * 2 * P], U8, name="w_words", align_bytes=64)
         w_scales = const.tile([P, BLOCKS * P], U8, name="w_scales", align_bytes=64)
         nc.vector.memset(w_scales[:].bitcast(I32), 0)
-        w_words = const.tile([P, BLOCKS * 2 * P], U8, name="w_words", align_bytes=64)
-        bias_rows = const.tile([P, P], BF16, name="bias_rows")
-        nc.vector.memset(bias_rows[:], 0.0)
 
         load(0)
-        weights = ((w_lin_words, w_lin_scales, b_lin), (w_gate_words, w_gate_scales, b_gate))
-        for i, (dram_words, dram_scales, dram_bias) in enumerate(weights):
-            nc.scalar.dma_start(out=bias_rows[2 * i : 2 * i + 2, :], in_=dram_bias.rearrange("(r c) -> r c", c=P))
+        load(1)
+        for i, (dram_words, dram_scales) in enumerate(((w_lin_words, w_lin_scales), (w_gate_words, w_gate_scales))):
             nc.sync.dma_start(
                 out=w_words[:, 2 * D * i : 2 * D * (i + 1)].bitcast(I32), in_=dram_words[0].bitcast(I32)
             )
@@ -165,21 +179,13 @@ def tile_scan_pb_t_kernel(
                     out=w_scales[32 * quad : 32 * quad + 4, D * i : D * (i + 1)].bitcast(I32),
                     in_=dram_scales[0, 4 * quad : 4 * quad + 4, :].bitcast(I32),
                 )
-        for r in range(1, LOAD_AHEAD):
+        for r in range(2, LOAD_AHEAD):
             load(r)
-
-        bias_f32 = const.tile([P, P], F32, name="bias_f32")
-        nc.vector.tensor_copy(out=bias_f32[:], in_=bias_rows[:])
-        bias_t = back_psum.tile([P, P], F32, name="bias_t", tag="bank")
-        nc.tensor.transpose(bias_t[:], bias_f32[:], ident[:])
-        bias_col = const.tile([P, BLOCKS], F32, name="bias_col")
-        nc.vector.tensor_copy(out=bias_col[:, 0:2], in_=bias_t[:, 0:2])
-        nc.vector.tensor_scalar_mul(out=bias_col[:, 2:4], in0=bias_t[:, 2:4], scalar1=-1.0)
 
         def live(c):
             return 0 <= c < HALF_ROUNDS
 
-        for h in range(-CAT_LEAD, HALF_ROUNDS + BACK_LAG):
+        def step(h):
             r, half = divmod(h, 2)
             if half == 0 and r + CAT_LEAD // 2 + LOAD_AHEAD < ROUNDS:
                 load(r + CAT_LEAD // 2 + LOAD_AHEAD)
@@ -195,3 +201,9 @@ def tile_scan_pb_t_kernel(
                 blend(h - BACK_LAG, upd, keep)
             if live(h + CAT_LEAD - 1):
                 quantise(h + CAT_LEAD - 1)
+
+        for h in range(-CAT_LEAD, -CAT_LEAD + 2):
+            step(h)
+        spread_biases()
+        for h in range(-CAT_LEAD + 2, HALF_ROUNDS + BACK_LAG):
+            step(h)

@@ -148,25 +148,17 @@ def tile_scan_pb_t_kernel(
                     nc.vector.tensor_tensor(out=result[:, jj, :], in0=change[:, jj, :], in1=q[:, jj, :], op=ALU.add)
             nc.sync.dma_start(out=out_rounds[r][:, tiles, :], in_=result[:])
 
-        def spread_biases():
-            bias_t = back_psum.tile([P, P], F32, name="bias_t", tag="bank")
-            nc.tensor.transpose(bias_t[:], bias_f32[:], ident[:])
-            nc.vector.tensor_copy(out=bias_col[:, 0:2], in_=bias_t[:, 0:2])
-            nc.vector.tensor_scalar_mul(out=bias_col[:, 2:4], in0=bias_t[:, 2:4], scalar1=-1.0)
-
-        bias_rows = const.tile([P, P], BF16, name="bias_rows")
-        bias_col = const.tile([P, BLOCKS], F32, name="bias_col")
-        nc.vector.memset(bias_rows[:], 0.0)
-        nc.gpsimd.dma_start(out=bias_rows[0:2, :], in_=b_lin.rearrange("(r c) -> r c", c=P))
-        nc.gpsimd.dma_start(out=bias_rows[2:4, :], in_=b_gate.rearrange("(r c) -> r c", c=P))
         ident = const.tile([P, P], F32, name="ident")
         make_identity(nc, ident[:])
-        bias_f32 = const.tile([P, P], F32, name="bias_f32")
-        nc.vector.tensor_copy(out=bias_f32[:], in_=bias_rows[:])
 
-        w_words = const.tile([P, BLOCKS * 2 * P], U8, name="w_words", align_bytes=64)
         w_scales = const.tile([P, BLOCKS * P], U8, name="w_scales", align_bytes=64)
         nc.vector.memset(w_scales[:].bitcast(I32), 0)
+        w_words = const.tile([P, BLOCKS * 2 * P], U8, name="w_words", align_bytes=64)
+        bias_rows = const.tile([P, P], BF16, name="bias_rows")
+        nc.vector.memset(bias_rows[:], 0.0)
+
+        nc.scalar.dma_start(out=bias_rows[0:2, :], in_=b_lin.rearrange("(r c) -> r c", c=P))
+        nc.scalar.dma_start(out=bias_rows[2:4, :], in_=b_gate.rearrange("(r c) -> r c", c=P))
 
         load(0)
         load(1)
@@ -182,10 +174,18 @@ def tile_scan_pb_t_kernel(
         for r in range(2, LOAD_AHEAD):
             load(r)
 
+        bias_f32 = const.tile([P, P], F32, name="bias_f32")
+        nc.vector.tensor_copy(out=bias_f32[:], in_=bias_rows[:])
+        bias_t = back_psum.tile([P, P], F32, name="bias_t", tag="bank")
+        nc.tensor.transpose(bias_t[:], bias_f32[:], ident[:])
+        bias_col = const.tile([P, BLOCKS], F32, name="bias_col")
+        nc.vector.tensor_copy(out=bias_col[:, 0:2], in_=bias_t[:, 0:2])
+        nc.vector.tensor_scalar_mul(out=bias_col[:, 2:4], in0=bias_t[:, 2:4], scalar1=-1.0)
+
         def live(c):
             return 0 <= c < HALF_ROUNDS
 
-        def step(h):
+        for h in range(-CAT_LEAD, HALF_ROUNDS + BACK_LAG):
             r, half = divmod(h, 2)
             if half == 0 and r + CAT_LEAD // 2 + LOAD_AHEAD < ROUNDS:
                 load(r + CAT_LEAD // 2 + LOAD_AHEAD)
@@ -201,9 +201,3 @@ def tile_scan_pb_t_kernel(
                 blend(h - BACK_LAG, upd, keep)
             if live(h + CAT_LEAD - 1):
                 quantise(h + CAT_LEAD - 1)
-
-        for h in range(-CAT_LEAD, -CAT_LEAD + 2):
-            step(h)
-        spread_biases()
-        for h in range(-CAT_LEAD + 2, HALF_ROUNDS + BACK_LAG):
-            step(h)

@@ -156,6 +156,8 @@ def tile_scan_pb_t_kernel(
         w_words = const.tile([P, BLOCKS * 2 * P], U8, name="w_words", align_bytes=64)
         bias_rows = const.tile([P, P], BF16, name="bias_rows")
         nc.vector.memset(bias_rows[:], 0.0)
+        table_probe = const.tile([P, 1], BF16, name="table_probe")
+        nc.scalar.activation(out=table_probe[:], in_=bias_rows[:, P - 1 : P], func=ACT.Tanh)
 
         nc.scalar.dma_start(out=bias_rows[0:2, :], in_=b_lin.rearrange("(r c) -> r c", c=P))
         nc.scalar.dma_start(out=bias_rows[2:4, :], in_=b_gate.rearrange("(r c) -> r c", c=P))
@@ -174,13 +176,15 @@ def tile_scan_pb_t_kernel(
         for r in range(2, LOAD_AHEAD):
             load(r)
 
-        bias_f32 = const.tile([P, P], F32, name="bias_f32")
-        nc.vector.tensor_copy(out=bias_f32[:], in_=bias_rows[:])
-        bias_t = back_psum.tile([P, P], F32, name="bias_t", tag="bank")
-        nc.tensor.transpose(bias_t[:], bias_f32[:], ident[:])
         bias_col = const.tile([P, BLOCKS], F32, name="bias_col")
-        nc.vector.tensor_copy(out=bias_col[:, 0:2], in_=bias_t[:, 0:2])
-        nc.vector.tensor_scalar_mul(out=bias_col[:, 2:4], in0=bias_t[:, 2:4], scalar1=-1.0)
+
+        def spread_biases():
+            bias_f32 = const.tile([P, P], F32, name="bias_f32")
+            nc.vector.tensor_copy(out=bias_f32[:], in_=bias_rows[:])
+            bias_t = back_psum.tile([P, P], F32, name="bias_t", tag="bank")
+            nc.tensor.transpose(bias_t[:], bias_f32[:], ident[:])
+            nc.vector.tensor_copy(out=bias_col[:, 0:2], in_=bias_t[:, 0:2])
+            nc.vector.tensor_scalar_mul(out=bias_col[:, 2:4], in0=bias_t[:, 2:4], scalar1=-1.0)
 
         def live(c):
             return 0 <= c < HALF_ROUNDS
@@ -201,3 +205,5 @@ def tile_scan_pb_t_kernel(
                 blend(h - BACK_LAG, upd, keep)
             if live(h + CAT_LEAD - 1):
                 quantise(h + CAT_LEAD - 1)
+            if h + CAT_LEAD == 1:
+                spread_biases()

@@ -60,8 +60,11 @@ def tile_scan_pb_t_kernel(
 
         def load(r):
             cat[r] = cat_pool.tile([P, TILES, K], BF16, name="cat")
-            nc.sync.dma_start(out=cat[r][:, :, 0:D], in_=q_rounds[r])
-            nc.sync.dma_start(out=cat[r][:, :, D:K], in_=wc_rounds[r])
+            pieces = 2 if r == 0 else 1
+            for i in range(pieces):
+                tiles = slice(i * TILES // pieces, (i + 1) * TILES // pieces)
+                nc.sync.dma_start(out=cat[r][:, tiles, 0:D], in_=q_rounds[r][:, tiles, :])
+                nc.sync.dma_start(out=cat[r][:, tiles, D:K], in_=wc_rounds[r][:, tiles, :])
 
         def transpose_cat(c):
             r, half = divmod(c, 2)
@@ -107,16 +110,19 @@ def tile_scan_pb_t_kernel(
 
         def activate(r, blocks):
             for b in blocks:
-                is_gate = b in GATE_BLOCKS
-                act = act_pool.tile([P, ROUND], F32, name="act", tag="act%d" % b)
-                nc.scalar.activation(
-                    out=act[:],
-                    in_=product[r, b][:],
-                    func=ACT.Sigmoid if is_gate else ACT.Tanh,
-                    bias=bias_col[:, b : b + 1],
-                    scale=-1.0 if is_gate else 1.0,
-                )
-                activated[r, b] = act
+                activated[r, b] = act_pool.tile([P, ROUND], F32, name="act", tag="act%d" % b)
+            pieces = 2 if r == ROUNDS - 1 else 1
+            for i in range(pieces):
+                tokens = slice(i * ROUND // pieces, (i + 1) * ROUND // pieces)
+                for b in blocks:
+                    is_gate = b in GATE_BLOCKS
+                    nc.scalar.activation(
+                        out=activated[r, b][:, tokens],
+                        in_=product[r, b][:, tokens],
+                        func=ACT.Sigmoid if is_gate else ACT.Tanh,
+                        bias=bias_col[:, b : b + 1],
+                        scale=-1.0 if is_gate else 1.0,
+                    )
 
         def transpose_back(c):
             r, half = divmod(c, 2)
@@ -143,10 +149,11 @@ def tile_scan_pb_t_kernel(
                 nc.vector.tensor_tensor(out=change[:, jj, :], in0=keep[:, jj, :], in1=diff[:, jj, :], op=ALU.mult)
             if c < HALF_ROUNDS - 1:
                 nc.gpsimd.tensor_tensor(out=result[:], in0=change[:], in1=q, op=ALU.add)
+                nc.sync.dma_start(out=out_rounds[r][:, tiles, :], in_=result[:])
             else:
                 for jj in range(2):
                     nc.vector.tensor_tensor(out=result[:, jj, :], in0=change[:, jj, :], in1=q[:, jj, :], op=ALU.add)
-            nc.sync.dma_start(out=out_rounds[r][:, tiles, :], in_=result[:])
+                    nc.sync.dma_start(out=out_rounds[r][:, 2 * half + jj, :], in_=result[:, jj, :])
 
         ident = const.tile([P, P], F32, name="ident")
         make_identity(nc, ident[:])
@@ -156,15 +163,13 @@ def tile_scan_pb_t_kernel(
         w_words = const.tile([P, BLOCKS * 2 * P], U8, name="w_words", align_bytes=64)
         bias_rows = const.tile([P, P], BF16, name="bias_rows")
         nc.vector.memset(bias_rows[:], 0.0)
-        table_probe = const.tile([P, 1], BF16, name="table_probe")
-        nc.scalar.activation(out=table_probe[:], in_=bias_rows[:, P - 1 : P], func=ACT.Tanh)
-
         nc.scalar.dma_start(out=bias_rows[0:2, :], in_=b_lin.rearrange("(r c) -> r c", c=P))
         nc.scalar.dma_start(out=bias_rows[2:4, :], in_=b_gate.rearrange("(r c) -> r c", c=P))
+        table_probe = const.tile([P, 2], F32, name="table_probe")
+        nc.vector.memset(table_probe[:], 0.0)
+        nc.scalar.activation(out=table_probe[:, 1:2], in_=table_probe[:, 0:1], func=ACT.Sigmoid)
 
-        load(0)
-        load(1)
-        for i, (dram_words, dram_scales) in enumerate(((w_lin_words, w_lin_scales), (w_gate_words, w_gate_scales))):
+        def load_weight(i, dram_words, dram_scales):
             nc.sync.dma_start(
                 out=w_words[:, 2 * D * i : 2 * D * (i + 1)].bitcast(I32), in_=dram_words[0].bitcast(I32)
             )
@@ -173,14 +178,21 @@ def tile_scan_pb_t_kernel(
                     out=w_scales[32 * quad : 32 * quad + 4, D * i : D * (i + 1)].bitcast(I32),
                     in_=dram_scales[0, 4 * quad : 4 * quad + 4, :].bitcast(I32),
                 )
-        for r in range(2, LOAD_AHEAD):
+
+        load(0)
+        load(1)
+        load_weight(0, w_lin_words, w_lin_scales)
+        load(2)
+        load_weight(1, w_gate_words, w_gate_scales)
+        for r in range(3, LOAD_AHEAD):
             load(r)
 
         bias_col = const.tile([P, BLOCKS], F32, name="bias_col")
 
+        bias_f32 = const.tile([P, P], F32, name="bias_f32")
+        nc.vector.tensor_copy(out=bias_f32[:], in_=bias_rows[:])
+
         def spread_biases():
-            bias_f32 = const.tile([P, P], F32, name="bias_f32")
-            nc.vector.tensor_copy(out=bias_f32[:], in_=bias_rows[:])
             bias_t = back_psum.tile([P, P], F32, name="bias_t", tag="bank")
             nc.tensor.transpose(bias_t[:], bias_f32[:], ident[:])
             nc.vector.tensor_copy(out=bias_col[:, 0:2], in_=bias_t[:, 0:2])

@@ -45,6 +45,7 @@ def tile_scan_pb_t_kernel(
         const = stack.enter_context(tc.tile_pool(name="const", bufs=1))
         cat_pool = stack.enter_context(tc.tile_pool(name="cat", bufs=ROUNDS))
         mx_pool = stack.enter_context(tc.tile_pool(name="mx", bufs=3))
+        split_pool = stack.enter_context(tc.tile_pool(name="split", bufs=3))
         act_pool = stack.enter_context(tc.tile_pool(name="act", bufs=2))
         blend_pool = stack.enter_context(tc.tile_pool(name="blend", bufs=4))
         cat_t_psum = stack.enter_context(tc.psum_pool(name="cat_t_psum", bufs=2))
@@ -53,6 +54,7 @@ def tile_scan_pb_t_kernel(
         stack.enter_context(tc.manual_schedule())
 
         cat = {}
+        split = {}
         grouped = {}
         codes = {}
         product = {}
@@ -66,13 +68,22 @@ def tile_scan_pb_t_kernel(
                 nc.sync.dma_start(out=cat[r][:, tiles, 0:D], in_=q_rounds[r][:, tiles, :])
                 nc.sync.dma_start(out=cat[r][:, tiles, D:K], in_=wc_rounds[r][:, tiles, :])
 
+        def split_words(c):
+            r, half = divmod(c, 2)
+            split[c] = split_pool.tile([P, 2, 2, P], F32, name="split")
+            nc.vector.tensor_copy(
+                out=split[c][:],
+                in_=cat[r][:, 2 * half : 2 * half + 2, :].bitcast(F32).rearrange("p j (w u) -> p j u w", u=2),
+            )
+
         def transpose_cat(c):
             r, half = divmod(c, 2)
             words_t = cat_t_psum.tile([P, 2, 2, P], F32, name="words_t")
             for jj in range(2):
                 words = cat[r][:, 2 * half + jj, :].bitcast(F32)
                 for u in range(2):
-                    nc.tensor.transpose(words_t[:, jj, u, :], words[:, u : K // 2 : 2], ident[:])
+                    source = words[:, u : K // 2 : 2] if c < CAT_LEAD else split[c][:, jj, u, :]
+                    nc.tensor.transpose(words_t[:, jj, u, :], source, ident[:])
             return words_t
 
         def regroup(c, words_t):
@@ -148,7 +159,8 @@ def tile_scan_pb_t_kernel(
             for jj in range(2):
                 nc.vector.tensor_tensor(out=change[:, jj, :], in0=keep[:, jj, :], in1=diff[:, jj, :], op=ALU.mult)
             if c < HALF_ROUNDS - 1:
-                nc.gpsimd.tensor_tensor(out=result[:], in0=change[:], in1=q, op=ALU.add)
+                for jj in range(2):
+                    nc.gpsimd.tensor_tensor(out=result[:, jj, :], in0=change[:, jj, :], in1=q[:, jj, :], op=ALU.add)
                 nc.sync.dma_start(out=out_rounds[r][:, tiles, :], in_=result[:])
             else:
                 for jj in range(2):
@@ -217,5 +229,7 @@ def tile_scan_pb_t_kernel(
                 blend(h - BACK_LAG, upd, keep)
             if live(h + CAT_LEAD - 1):
                 quantise(h + CAT_LEAD - 1)
+            if live(h + CAT_LEAD + 1) and h >= -1:
+                split_words(h + CAT_LEAD + 1)
             if h + CAT_LEAD == 1:
                 spread_biases()

@@ -27,6 +27,7 @@ LIN_BLOCKS = (0, 1)
 GATE_BLOCKS = (2, 3)
 LOAD_AHEAD = 4
 CAT_LEAD = 4
+SPLIT_LEAD = CAT_LEAD + 2
 BACK_LAG = 2
 
 FLOPS = 2 * TOKENS * K * (2 * D)
@@ -159,8 +160,7 @@ def tile_scan_pb_t_kernel(
             for jj in range(2):
                 nc.vector.tensor_tensor(out=change[:, jj, :], in0=keep[:, jj, :], in1=diff[:, jj, :], op=ALU.mult)
             if c < HALF_ROUNDS - 1:
-                for jj in range(2):
-                    nc.gpsimd.tensor_tensor(out=result[:, jj, :], in0=change[:, jj, :], in1=q[:, jj, :], op=ALU.add)
+                nc.gpsimd.tensor_tensor(out=result[:], in0=change[:], in1=q, op=ALU.add)
                 nc.sync.dma_start(out=out_rounds[r][:, tiles, :], in_=result[:])
             else:
                 for jj in range(2):
@@ -229,7 +229,7 @@ def tile_scan_pb_t_kernel(
                 blend(h - BACK_LAG, upd, keep)
             if live(h + CAT_LEAD - 1):
                 quantise(h + CAT_LEAD - 1)
-            if live(h + CAT_LEAD + 1) and h >= -1:
-                split_words(h + CAT_LEAD + 1)
+            if live(h + SPLIT_LEAD) and h + SPLIT_LEAD >= CAT_LEAD:
+                split_words(h + SPLIT_LEAD)
             if h + CAT_LEAD == 1:
                 spread_biases()

@@ -27,6 +27,7 @@ LIN_BLOCKS = (0, 1)
 GATE_BLOCKS = (2, 3)
 LOAD_AHEAD = 4
 CAT_LEAD = 4
+FIRST_SPLIT = 6
 SPLIT_LEAD = CAT_LEAD + 2
 BACK_LAG = 2
 
@@ -45,7 +46,7 @@ def tile_scan_pb_t_kernel(
     with ExitStack() as stack:
         const = stack.enter_context(tc.tile_pool(name="const", bufs=1))
         cat_pool = stack.enter_context(tc.tile_pool(name="cat", bufs=ROUNDS))
-        mx_pool = stack.enter_context(tc.tile_pool(name="mx", bufs=3))
+        mx_pool = stack.enter_context(tc.tile_pool(name="mx", bufs=4))
         split_pool = stack.enter_context(tc.tile_pool(name="split", bufs=3))
         act_pool = stack.enter_context(tc.tile_pool(name="act", bufs=2))
         blend_pool = stack.enter_context(tc.tile_pool(name="blend", bufs=4))
@@ -61,20 +62,18 @@ def tile_scan_pb_t_kernel(
         product = {}
         activated = {}
 
-        def load(r):
-            cat[r] = cat_pool.tile([P, TILES, K], BF16, name="cat")
-            pieces = 2 if r == 0 else 1
-            for i in range(pieces):
-                tiles = slice(i * TILES // pieces, (i + 1) * TILES // pieces)
-                nc.sync.dma_start(out=cat[r][:, tiles, 0:D], in_=q_rounds[r][:, tiles, :])
-                nc.sync.dma_start(out=cat[r][:, tiles, D:K], in_=wc_rounds[r][:, tiles, :])
+        def load(r, tiles=slice(0, TILES)):
+            if r not in cat:
+                cat[r] = cat_pool.tile([P, TILES, K], BF16, name="cat")
+            nc.sync.dma_start(out=cat[r][:, tiles, 0:D], in_=q_rounds[r][:, tiles, :])
+            nc.sync.dma_start(out=cat[r][:, tiles, D:K], in_=wc_rounds[r][:, tiles, :])
 
         def split_words(c):
             r, half = divmod(c, 2)
             split[c] = split_pool.tile([P, 2, 2, P], F32, name="split")
             nc.vector.tensor_copy(
-                out=split[c][:],
-                in_=cat[r][:, 2 * half : 2 * half + 2, :].bitcast(F32).rearrange("p j (w u) -> p j u w", u=2),
+                out=split[c][:].rearrange("p j u w -> p j w u"),
+                in_=cat[r][:, 2 * half : 2 * half + 2, :].bitcast(F32).rearrange("p j (w u) -> p j w u", u=2),
             )
 
         def transpose_cat(c):
@@ -83,13 +82,14 @@ def tile_scan_pb_t_kernel(
             for jj in range(2):
                 words = cat[r][:, 2 * half + jj, :].bitcast(F32)
                 for u in range(2):
-                    source = words[:, u : K // 2 : 2] if c < CAT_LEAD else split[c][:, jj, u, :]
+                    source = words[:, u : K // 2 : 2] if c < FIRST_SPLIT else split[c][:, jj, u, :]
                     nc.tensor.transpose(words_t[:, jj, u, :], source, ident[:])
             return words_t
 
-        def regroup(c, words_t):
+        def regroup(c, words_t, on_vector=False):
             grouped[c] = mx_pool.tile([P, 2, P, 4], BF16, name="grouped", align_bytes=64)
-            nc.scalar.copy(out=grouped[c][:].bitcast(F32), in_=words_t[:].rearrange("p j u t -> p j t u"))
+            copy = nc.vector.tensor_copy if on_vector else nc.scalar.copy
+            copy(out=grouped[c][:].bitcast(F32), in_=words_t[:].rearrange("p j u t -> p j t u"))
 
         def quantise(c):
             r, half = divmod(c, 2)
@@ -175,8 +175,6 @@ def tile_scan_pb_t_kernel(
         w_words = const.tile([P, BLOCKS * 2 * P], U8, name="w_words", align_bytes=64)
         bias_rows = const.tile([P, P], BF16, name="bias_rows")
         nc.vector.memset(bias_rows[:], 0.0)
-        nc.scalar.dma_start(out=bias_rows[0:2, :], in_=b_lin.rearrange("(r c) -> r c", c=P))
-        nc.scalar.dma_start(out=bias_rows[2:4, :], in_=b_gate.rearrange("(r c) -> r c", c=P))
         table_probe = const.tile([P, 2], F32, name="table_probe")
         nc.vector.memset(table_probe[:], 0.0)
         nc.scalar.activation(out=table_probe[:, 1:2], in_=table_probe[:, 0:1], func=ACT.Sigmoid)
@@ -191,7 +189,10 @@ def tile_scan_pb_t_kernel(
                     in_=dram_scales[0, 4 * quad : 4 * quad + 4, :].bitcast(I32),
                 )
 
-        load(0)
+        load(0, slice(0, 2))
+        nc.sync.dma_start(out=bias_rows[0:2, :], in_=b_lin.rearrange("(r c) -> r c", c=P))
+        nc.sync.dma_start(out=bias_rows[2:4, :], in_=b_gate.rearrange("(r c) -> r c", c=P))
+        load(0, slice(2, 4))
         load(1)
         load_weight(0, w_lin_words, w_lin_scales)
         load(2)
@@ -213,23 +214,40 @@ def tile_scan_pb_t_kernel(
         def live(c):
             return 0 <= c < HALF_ROUNDS
 
-        for h in range(-CAT_LEAD, HALF_ROUNDS + BACK_LAG):
+        regroup(0, transpose_cat(0))
+        regroup(1, transpose_cat(1))
+        spread_biases()
+        quantise(0)
+        quantise(1)
+        regroup(2, transpose_cat(2))
+        regroup(3, transpose_cat(3), on_vector=True)
+        multiply(0, LIN_BLOCKS)
+        activate(0, LIN_BLOCKS)
+        quantise(2)
+        quantise(3)
+        multiply(0, GATE_BLOCKS)
+        activate(0, GATE_BLOCKS)
+        split_words(6)
+        regroup(4, transpose_cat(4), on_vector=True)
+        regroup(5, transpose_cat(5))
+        quantise(4)
+        split_words(7)
+        for r in range(LOAD_AHEAD, LOAD_AHEAD + 2):
+            load(r)
+        for h in range(2, HALF_ROUNDS + BACK_LAG):
             r, half = divmod(h, 2)
-            if half == 0 and r + CAT_LEAD // 2 + LOAD_AHEAD < ROUNDS:
-                load(r + CAT_LEAD // 2 + LOAD_AHEAD)
+            if half == 0 and r + CAT_LEAD // 2 + LOAD_AHEAD - 1 < ROUNDS:
+                load(r + CAT_LEAD // 2 + LOAD_AHEAD - 1)
             if live(h):
                 blocks = LIN_BLOCKS if half == 0 else GATE_BLOCKS
                 multiply(r, blocks)
                 activate(r, blocks)
-            if live(h + CAT_LEAD):
-                words_t = transpose_cat(h + CAT_LEAD)
-                regroup(h + CAT_LEAD, words_t)
             if live(h - BACK_LAG):
                 upd, keep = transpose_back(h - BACK_LAG)
                 blend(h - BACK_LAG, upd, keep)
+            if live(h + CAT_LEAD):
+                regroup(h + CAT_LEAD, transpose_cat(h + CAT_LEAD))
             if live(h + CAT_LEAD - 1):
                 quantise(h + CAT_LEAD - 1)
-            if live(h + SPLIT_LEAD) and h + SPLIT_LEAD >= CAT_LEAD:
+            if live(h + SPLIT_LEAD):
                 split_words(h + SPLIT_LEAD)
-            if h + CAT_LEAD == 1:
-                spread_biases()

@@ -25,10 +25,12 @@ HALF_ROUNDS = 2 * ROUNDS
 BLOCKS = 4
 LIN_BLOCKS = (0, 1)
 GATE_BLOCKS = (2, 3)
-LOAD_AHEAD = 4
+LOAD_AHEAD = 8
 CAT_LEAD = 4
 FIRST_SPLIT = 6
 SPLIT_LEAD = CAT_LEAD + 2
+LAST_WHOLE = ROUNDS - 3
+WARM_UP = 4
 BACK_LAG = 2
 
 FLOPS = 2 * TOKENS * K * (2 * D)
@@ -47,12 +49,10 @@ def tile_scan_pb_t_kernel(
         const = stack.enter_context(tc.tile_pool(name="const", bufs=1))
         cat_pool = stack.enter_context(tc.tile_pool(name="cat", bufs=ROUNDS))
         mx_pool = stack.enter_context(tc.tile_pool(name="mx", bufs=4))
-        split_pool = stack.enter_context(tc.tile_pool(name="split", bufs=3))
+        split_pool = stack.enter_context(tc.tile_pool(name="split", bufs=6))
         act_pool = stack.enter_context(tc.tile_pool(name="act", bufs=2))
         blend_pool = stack.enter_context(tc.tile_pool(name="blend", bufs=4))
-        cat_t_psum = stack.enter_context(tc.psum_pool(name="cat_t_psum", bufs=2))
-        product_psum = stack.enter_context(tc.psum_pool(name="product_psum", bufs=3))
-        back_psum = stack.enter_context(tc.psum_pool(name="back_psum", bufs=3))
+        psum = stack.enter_context(tc.psum_pool(name="psum", bufs=8))
         stack.enter_context(tc.manual_schedule())
 
         cat = {}
@@ -60,6 +60,7 @@ def tile_scan_pb_t_kernel(
         grouped = {}
         codes = {}
         product = {}
+        change = {}
         activated = {}
 
         def load(r, tiles=slice(0, TILES)):
@@ -78,7 +79,7 @@ def tile_scan_pb_t_kernel(
 
         def transpose_cat(c):
             r, half = divmod(c, 2)
-            words_t = cat_t_psum.tile([P, 2, 2, P], F32, name="words_t")
+            words_t = psum.tile([P, 2, 2, P], F32, name="words_t", tag="bank")
             for jj in range(2):
                 words = cat[r][:, 2 * half + jj, :].bitcast(F32)
                 for u in range(2):
@@ -108,7 +109,7 @@ def tile_scan_pb_t_kernel(
         def multiply(r, blocks):
             code_words, code_scales = codes[r]
             for b in blocks:
-                acc = product_psum.tile([P, ROUND], F32, name="acc")
+                acc = psum.tile([P, ROUND], F32, name="acc", tag="bank")
                 nc.tensor.matmul_mx(
                     out=acc[:],
                     lhsT=w_words[:, 2 * P * b : 2 * P * (b + 1)].bitcast(FP4X4),
@@ -140,7 +141,7 @@ def tile_scan_pb_t_kernel(
             r, half = divmod(c, 2)
             banks = []
             for blocks in (LIN_BLOCKS, GATE_BLOCKS):
-                bank = back_psum.tile([P, 2, D], F32, name="bank")
+                bank = psum.tile([P, 2, D], F32, name="bank", tag="bank")
                 for jj in range(2):
                     tokens = slice(P * (2 * half + jj), P * (2 * half + jj + 1))
                     for i, b in enumerate(blocks):
@@ -150,22 +151,22 @@ def tile_scan_pb_t_kernel(
 
         def blend(c, upd, keep):
             r, half = divmod(c, 2)
-            tiles = slice(2 * half, 2 * half + 2)
-            q = cat[r][:, tiles, 0:D]
+            if half == 0:
+                change[r] = blend_pool.tile([P, TILES, D], F32, name="change")
             diff = blend_pool.tile([P, 2, D], F32, name="diff")
-            change = blend_pool.tile([P, 2, D], F32, name="change")
-            result = blend_pool.tile([P, 2, D], F32, name="result")
             for jj in range(2):
-                nc.vector.tensor_tensor(out=diff[:, jj, :], in0=upd[:, jj, :], in1=q[:, jj, :], op=ALU.subtract)
+                q = cat[r][:, 2 * half + jj, 0:D]
+                nc.vector.tensor_tensor(out=diff[:, jj, :], in0=upd[:, jj, :], in1=q, op=ALU.subtract)
             for jj in range(2):
-                nc.vector.tensor_tensor(out=change[:, jj, :], in0=keep[:, jj, :], in1=diff[:, jj, :], op=ALU.mult)
-            if c < HALF_ROUNDS - 1:
-                nc.gpsimd.tensor_tensor(out=result[:], in0=change[:], in1=q, op=ALU.add)
-                nc.sync.dma_start(out=out_rounds[r][:, tiles, :], in_=result[:])
-            else:
-                for jj in range(2):
-                    nc.vector.tensor_tensor(out=result[:, jj, :], in0=change[:, jj, :], in1=q[:, jj, :], op=ALU.add)
-                    nc.sync.dma_start(out=out_rounds[r][:, 2 * half + jj, :], in_=result[:, jj, :])
+                moved = change[r][:, 2 * half + jj, :]
+                nc.vector.tensor_tensor(out=moved, in0=keep[:, jj, :], in1=diff[:, jj, :], op=ALU.mult)
+
+        def add_query(engine, r, tiles):
+            result = blend_pool.tile([P, TILES, D], F32, name="result")
+            engine.tensor_tensor(
+                out=result[:, tiles, :], in0=change[r][:, tiles, :], in1=cat[r][:, tiles, 0:D], op=ALU.add
+            )
+            nc.sync.dma_start(out=out_rounds[r][:, tiles, :], in_=result[:, tiles, :])
 
         ident = const.tile([P, P], F32, name="ident")
         make_identity(nc, ident[:])
@@ -178,6 +179,12 @@ def tile_scan_pb_t_kernel(
         table_probe = const.tile([P, 2], F32, name="table_probe")
         nc.vector.memset(table_probe[:], 0.0)
         nc.scalar.activation(out=table_probe[:, 1:2], in_=table_probe[:, 0:1], func=ACT.Sigmoid)
+
+        idle_rows = const.tile([P, ROUND], BF16, name="idle_rows")
+        nc.vector.memset(idle_rows[:], 0.0)
+        for i in range(WARM_UP):
+            idle_bank = psum.tile([P, ROUND], F32, name="idle_bank", tag="bank")
+            nc.tensor.matmul(idle_bank[:], lhsT=idle_rows[:, 0:P], rhs=idle_rows[:], start=True, stop=True)
 
         def load_weight(i, dram_words, dram_scales):
             nc.sync.dma_start(
@@ -197,7 +204,7 @@ def tile_scan_pb_t_kernel(
         load_weight(0, w_lin_words, w_lin_scales)
         load(2)
         load_weight(1, w_gate_words, w_gate_scales)
-        for r in range(3, LOAD_AHEAD):
+        for r in range(3, LOAD_AHEAD + 1):
             load(r)
 
         bias_col = const.tile([P, BLOCKS], F32, name="bias_col")
@@ -206,7 +213,7 @@ def tile_scan_pb_t_kernel(
         nc.vector.tensor_copy(out=bias_f32[:], in_=bias_rows[:])
 
         def spread_biases():
-            bias_t = back_psum.tile([P, P], F32, name="bias_t", tag="bank")
+            bias_t = psum.tile([P, P], F32, name="bias_t", tag="bank")
             nc.tensor.transpose(bias_t[:], bias_f32[:], ident[:])
             nc.vector.tensor_copy(out=bias_col[:, 0:2], in_=bias_t[:, 0:2])
             nc.vector.tensor_scalar_mul(out=bias_col[:, 2:4], in0=bias_t[:, 2:4], scalar1=-1.0)
@@ -229,25 +236,35 @@ def tile_scan_pb_t_kernel(
         activate(0, GATE_BLOCKS)
         split_words(6)
         regroup(4, transpose_cat(4), on_vector=True)
-        regroup(5, transpose_cat(5))
-        quantise(4)
         split_words(7)
-        for r in range(LOAD_AHEAD, LOAD_AHEAD + 2):
-            load(r)
-        for h in range(2, HALF_ROUNDS + BACK_LAG):
-            r, half = divmod(h, 2)
-            if half == 0 and r + CAT_LEAD // 2 + LOAD_AHEAD - 1 < ROUNDS:
-                load(r + CAT_LEAD // 2 + LOAD_AHEAD - 1)
-            if live(h):
-                blocks = LIN_BLOCKS if half == 0 else GATE_BLOCKS
-                multiply(r, blocks)
-                activate(r, blocks)
-            if live(h - BACK_LAG):
-                upd, keep = transpose_back(h - BACK_LAG)
-                blend(h - BACK_LAG, upd, keep)
-            if live(h + CAT_LEAD):
-                regroup(h + CAT_LEAD, transpose_cat(h + CAT_LEAD))
-            if live(h + CAT_LEAD - 1):
-                quantise(h + CAT_LEAD - 1)
-            if live(h + SPLIT_LEAD):
-                split_words(h + SPLIT_LEAD)
+        words_t = transpose_cat(5)
+        for r in range(1, ROUNDS + 1):
+            if r + LOAD_AHEAD < ROUNDS:
+                load(r + LOAD_AHEAD)
+            if live(2 * r + 3):
+                regroup(2 * r + 3, words_t)
+            if live(2 * r + 2):
+                quantise(2 * r + 2)
+            for c in (2 * r, 2 * r + 1):
+                if live(c + 6):
+                    split_words(c + 6)
+            if live(2 * r + 2):
+                quantise(2 * r + 3)
+            for c in (2 * r, 2 * r + 1):
+                if r < ROUNDS:
+                    blocks = GATE_BLOCKS if c % 2 else LIN_BLOCKS
+                    multiply(r, blocks)
+                    activate(r, blocks)
+                upd, keep = transpose_back(c - 2)
+                blend(c - 2, upd, keep)
+                if live(c + 4):
+                    words_t = transpose_cat(c + 4)
+                    if c == 2 * r:
+                        regroup(c + 4, words_t)
+                if r == ROUNDS and c % 2:
+                    add_query(nc.vector, r - 1, slice(2, 3))
+                    add_query(nc.vector, r - 1, slice(3, 4))
+                elif r >= LAST_WHOLE:
+                    add_query(nc.gpsimd, r - 1, slice(c % 2 * 2, c % 2 * 2 + 2))
+            if r < LAST_WHOLE:
+                add_query(nc.gpsimd, r - 1, slice(0, TILES))

@@ -29,8 +29,10 @@ LOAD_AHEAD = 8
 CAT_LEAD = 4
 FIRST_SPLIT = 6
 SPLIT_LEAD = CAT_LEAD + 2
-LAST_WHOLE = ROUNDS - 3
+LAST_WHOLE = ROUNDS - 2
+BRIDGE = 64
 WARM_UP = 4
+SPLIT_TILES = 2
 BACK_LAG = 2
 
 FLOPS = 2 * TOKENS * K * (2 * D)
@@ -49,10 +51,12 @@ def tile_scan_pb_t_kernel(
         const = stack.enter_context(tc.tile_pool(name="const", bufs=1))
         cat_pool = stack.enter_context(tc.tile_pool(name="cat", bufs=ROUNDS))
         mx_pool = stack.enter_context(tc.tile_pool(name="mx", bufs=4))
-        split_pool = stack.enter_context(tc.tile_pool(name="split", bufs=6))
+        split_pool = stack.enter_context(tc.tile_pool(name="split", bufs=3))
         act_pool = stack.enter_context(tc.tile_pool(name="act", bufs=2))
-        blend_pool = stack.enter_context(tc.tile_pool(name="blend", bufs=4))
-        psum = stack.enter_context(tc.psum_pool(name="psum", bufs=8))
+        blend_pool = stack.enter_context(tc.tile_pool(name="blend", bufs=6))
+        cat_t_psum = stack.enter_context(tc.psum_pool(name="cat_t_psum", bufs=1))
+        product_psum = stack.enter_context(tc.psum_pool(name="product_psum", bufs=3))
+        back_psum = stack.enter_context(tc.psum_pool(name="back_psum", bufs=4))
         stack.enter_context(tc.manual_schedule())
 
         cat = {}
@@ -60,6 +64,7 @@ def tile_scan_pb_t_kernel(
         grouped = {}
         codes = {}
         product = {}
+        pending = {}
         change = {}
         activated = {}
 
@@ -69,47 +74,58 @@ def tile_scan_pb_t_kernel(
             nc.sync.dma_start(out=cat[r][:, tiles, 0:D], in_=q_rounds[r][:, tiles, :])
             nc.sync.dma_start(out=cat[r][:, tiles, D:K], in_=wc_rounds[r][:, tiles, :])
 
-        def split_words(c):
-            r, half = divmod(c, 2)
-            split[c] = split_pool.tile([P, 2, 2, P], F32, name="split")
+        def split_words(r):
+            split[r] = split_pool.tile([P, SPLIT_TILES, 2, P], F32, name="split")
             nc.vector.tensor_copy(
-                out=split[c][:].rearrange("p j u w -> p j w u"),
-                in_=cat[r][:, 2 * half : 2 * half + 2, :].bitcast(F32).rearrange("p j (w u) -> p j w u", u=2),
+                out=split[r][:].rearrange("p j u w -> p j w u"),
+                in_=cat[r][:, 0:SPLIT_TILES, :].bitcast(F32).rearrange("p j (w u) -> p j w u", u=2),
             )
 
         def transpose_cat(c):
             r, half = divmod(c, 2)
-            words_t = psum.tile([P, 2, 2, P], F32, name="words_t", tag="bank")
+            if c < FIRST_SPLIT and c % 2 == 1:
+                words_t = back_psum.tile([P, 2, 2, P], F32, name="words_t", tag="bank")
+            else:
+                words_t = cat_t_psum.tile([P, 2, 2, P], F32, name="words_t")
             for jj in range(2):
-                words = cat[r][:, 2 * half + jj, :].bitcast(F32)
+                j = 2 * half + jj
+                words = cat[r][:, j, :].bitcast(F32)
                 for u in range(2):
-                    source = words[:, u : K // 2 : 2] if c < FIRST_SPLIT else split[c][:, jj, u, :]
+                    apart = r in split and j < SPLIT_TILES
+                    source = split[r][:, j, u, :] if apart else words[:, u : K // 2 : 2]
                     nc.tensor.transpose(words_t[:, jj, u, :], source, ident[:])
             return words_t
 
         def regroup(c, words_t, on_vector=False):
-            grouped[c] = mx_pool.tile([P, 2, P, 4], BF16, name="grouped", align_bytes=64)
-            copy = nc.vector.tensor_copy if on_vector else nc.scalar.copy
-            copy(out=grouped[c][:].bitcast(F32), in_=words_t[:].rearrange("p j u t -> p j t u"))
-
-        def quantise(c):
             r, half = divmod(c, 2)
             if half == 0:
+                grouped[r] = mx_pool.tile([P, TILES, P, 4], BF16, name="grouped", align_bytes=64)
+            words = grouped[r][:, 2 * half : 2 * half + 2, :, :].bitcast(F32)
+            copy = nc.vector.tensor_copy if on_vector else nc.scalar.copy
+            copy(out=words, in_=words_t[:].rearrange("p j u t -> p j t u"))
+
+        def quantise(r, tiles=slice(0, TILES)):
+            if r not in codes:
                 code_words = mx_pool.tile([P, ROUND], U32, name="code_words", align_bytes=64)
                 code_scales = mx_pool.tile([P, ROUND], U8, name="code_scales", align_bytes=64)
                 codes[r] = (code_words, code_scales)
             code_words, code_scales = codes[r]
-            tokens = slice(HALF * half, HALF * (half + 1))
+            tokens = slice(P * tiles.start, P * tiles.stop)
             nc.vector.quantize_mx(
                 out=code_words[:, tokens].bitcast(FP8X4),
                 scales=code_scales[:, tokens],
-                in_=grouped[c][:].rearrange("p j t k -> p (j t k)"),
+                in_=grouped[r][:, tiles, :, :].rearrange("p j t k -> p (j t k)"),
             )
+
+        def bridge(columns):
+            nc.tensor.matmul(columns, lhsT=idle_rows[:, 0:P], rhs=idle_rows[:, 0:BRIDGE], start=True, stop=True)
 
         def multiply(r, blocks):
             code_words, code_scales = codes[r]
             for b in blocks:
-                acc = psum.tile([P, ROUND], F32, name="acc", tag="bank")
+                acc = product_psum.tile([P, ROUND], F32, name="acc")
+                if b == blocks[0]:
+                    bridge(acc[:, 0:BRIDGE])
                 nc.tensor.matmul_mx(
                     out=acc[:],
                     lhsT=w_words[:, 2 * P * b : 2 * P * (b + 1)].bitcast(FP4X4),
@@ -141,7 +157,9 @@ def tile_scan_pb_t_kernel(
             r, half = divmod(c, 2)
             banks = []
             for blocks in (LIN_BLOCKS, GATE_BLOCKS):
-                bank = psum.tile([P, 2, D], F32, name="bank", tag="bank")
+                bank = back_psum.tile([P, 2, D], F32, name="bank")
+                if blocks == LIN_BLOCKS:
+                    bridge(bank[:, 0, 0:BRIDGE])
                 for jj in range(2):
                     tokens = slice(P * (2 * half + jj), P * (2 * half + jj + 1))
                     for i, b in enumerate(blocks):
@@ -149,17 +167,20 @@ def tile_scan_pb_t_kernel(
                 banks.append(bank)
             return banks
 
-        def blend(c, upd, keep):
+        def start_blend(c, upd, keep):
+            r, half = divmod(c, 2)
+            diff = blend_pool.tile([P, 2, D], F32, name="diff")
+            q = cat[r][:, 2 * half : 2 * half + 2, 0:D]
+            nc.vector.tensor_tensor(out=diff[:], in0=upd[:], in1=q, op=ALU.subtract)
+            pending[c] = (diff, keep)
+
+        def end_blend(c):
             r, half = divmod(c, 2)
             if half == 0:
                 change[r] = blend_pool.tile([P, TILES, D], F32, name="change")
-            diff = blend_pool.tile([P, 2, D], F32, name="diff")
-            for jj in range(2):
-                q = cat[r][:, 2 * half + jj, 0:D]
-                nc.vector.tensor_tensor(out=diff[:, jj, :], in0=upd[:, jj, :], in1=q, op=ALU.subtract)
-            for jj in range(2):
-                moved = change[r][:, 2 * half + jj, :]
-                nc.vector.tensor_tensor(out=moved, in0=keep[:, jj, :], in1=diff[:, jj, :], op=ALU.mult)
+            diff, keep = pending.pop(c)
+            moved = change[r][:, 2 * half : 2 * half + 2, :]
+            nc.vector.tensor_tensor(out=moved, in0=keep[:], in1=diff[:], op=ALU.mult)
 
         def add_query(engine, r, tiles):
             result = blend_pool.tile([P, TILES, D], F32, name="result")
@@ -183,7 +204,7 @@ def tile_scan_pb_t_kernel(
         idle_rows = const.tile([P, ROUND], BF16, name="idle_rows")
         nc.vector.memset(idle_rows[:], 0.0)
         for i in range(WARM_UP):
-            idle_bank = psum.tile([P, ROUND], F32, name="idle_bank", tag="bank")
+            idle_bank = product_psum.tile([P, ROUND], F32, name="idle_bank", tag="acc")
             nc.tensor.matmul(idle_bank[:], lhsT=idle_rows[:, 0:P], rhs=idle_rows[:], start=True, stop=True)
 
         def load_weight(i, dram_words, dram_scales):
@@ -213,7 +234,7 @@ def tile_scan_pb_t_kernel(
         nc.vector.tensor_copy(out=bias_f32[:], in_=bias_rows[:])
 
         def spread_biases():
-            bias_t = psum.tile([P, P], F32, name="bias_t", tag="bank")
+            bias_t = back_psum.tile([P, P], F32, name="bias_t", tag="bank")
             nc.tensor.transpose(bias_t[:], bias_f32[:], ident[:])
             nc.vector.tensor_copy(out=bias_col[:, 0:2], in_=bias_t[:, 0:2])
             nc.vector.tensor_scalar_mul(out=bias_col[:, 2:4], in0=bias_t[:, 2:4], scalar1=-1.0)
@@ -224,47 +245,45 @@ def tile_scan_pb_t_kernel(
         regroup(0, transpose_cat(0))
         regroup(1, transpose_cat(1))
         spread_biases()
-        quantise(0)
-        quantise(1)
+        quantise(0, slice(0, 2))
+        quantise(0, slice(2, 4))
         regroup(2, transpose_cat(2))
         regroup(3, transpose_cat(3), on_vector=True)
         multiply(0, LIN_BLOCKS)
         activate(0, LIN_BLOCKS)
-        quantise(2)
-        quantise(3)
+        quantise(1)
         multiply(0, GATE_BLOCKS)
         activate(0, GATE_BLOCKS)
-        split_words(6)
         regroup(4, transpose_cat(4), on_vector=True)
-        split_words(7)
+        split_words(3)
         words_t = transpose_cat(5)
         for r in range(1, ROUNDS + 1):
             if r + LOAD_AHEAD < ROUNDS:
                 load(r + LOAD_AHEAD)
-            if live(2 * r + 3):
+            if r + 1 < ROUNDS:
                 regroup(2 * r + 3, words_t)
-            if live(2 * r + 2):
-                quantise(2 * r + 2)
-            for c in (2 * r, 2 * r + 1):
-                if live(c + 6):
-                    split_words(c + 6)
-            if live(2 * r + 2):
-                quantise(2 * r + 3)
+                quantise(r + 1)
+            if r + 3 < ROUNDS:
+                split_words(r + 3)
             for c in (2 * r, 2 * r + 1):
                 if r < ROUNDS:
                     blocks = GATE_BLOCKS if c % 2 else LIN_BLOCKS
                     multiply(r, blocks)
                     activate(r, blocks)
                 upd, keep = transpose_back(c - 2)
-                blend(c - 2, upd, keep)
-                if live(c + 4):
+                start_blend(c - 2, upd, keep)
+                if r + 2 < ROUNDS:
                     words_t = transpose_cat(c + 4)
                     if c == 2 * r:
                         regroup(c + 4, words_t)
-                if r == ROUNDS and c % 2:
-                    add_query(nc.vector, r - 1, slice(2, 3))
-                    add_query(nc.vector, r - 1, slice(3, 4))
-                elif r >= LAST_WHOLE:
-                    add_query(nc.gpsimd, r - 1, slice(c % 2 * 2, c % 2 * 2 + 2))
-            if r < LAST_WHOLE:
+            end_blend(2 * r - 2)
+            if r >= LAST_WHOLE:
+                add_query(nc.gpsimd, r - 1, slice(0, 2))
+            end_blend(2 * r - 1)
+            if r == ROUNDS:
+                add_query(nc.vector, r - 1, slice(2, 3))
+                add_query(nc.vector, r - 1, slice(3, 4))
+            elif r >= LAST_WHOLE:
+                add_query(nc.gpsimd, r - 1, slice(2, 4))
+            else:
                 add_query(nc.gpsimd, r - 1, slice(0, TILES))

@@ -31,8 +31,8 @@ FIRST_SPLIT = 6
 SPLIT_LEAD = CAT_LEAD + 2
 LAST_WHOLE = ROUNDS - 2
 BRIDGE = 64
-WARM_UP = 4
-SPLIT_TILES = 2
+WARM_UP = 3
+SPLIT_TILES = 3
 BACK_LAG = 2
 
 FLOPS = 2 * TOKENS * K * (2 * D)
@@ -75,10 +75,10 @@ def tile_scan_pb_t_kernel(
             nc.sync.dma_start(out=cat[r][:, tiles, D:K], in_=wc_rounds[r][:, tiles, :])
 
         def split_words(r):
-            split[r] = split_pool.tile([P, SPLIT_TILES, 2, P], F32, name="split")
+            split[r] = split_pool.tile([P, 2, SPLIT_TILES, P], F32, name="split")
             nc.vector.tensor_copy(
-                out=split[r][:].rearrange("p j u w -> p j w u"),
-                in_=cat[r][:, 0:SPLIT_TILES, :].bitcast(F32).rearrange("p j (w u) -> p j w u", u=2),
+                out=split[r][:].rearrange("p u j w -> p (j w) u"),
+                in_=cat[r][:, 0:SPLIT_TILES, :].bitcast(F32).rearrange("p j (w u) -> p (j w) u", u=2),
             )
 
         def transpose_cat(c):
@@ -92,7 +92,7 @@ def tile_scan_pb_t_kernel(
                 words = cat[r][:, j, :].bitcast(F32)
                 for u in range(2):
                     apart = r in split and j < SPLIT_TILES
-                    source = split[r][:, j, u, :] if apart else words[:, u : K // 2 : 2]
+                    source = split[r][:, u, j, :] if apart else words[:, u : K // 2 : 2]
                     nc.tensor.transpose(words_t[:, jj, u, :], source, ident[:])
             return words_t
 
@@ -193,16 +193,16 @@ def tile_scan_pb_t_kernel(
         make_identity(nc, ident[:])
 
         w_scales = const.tile([P, BLOCKS * P], U8, name="w_scales", align_bytes=64)
-        nc.vector.memset(w_scales[:].bitcast(I32), 0)
         w_words = const.tile([P, BLOCKS * 2 * P], U8, name="w_words", align_bytes=64)
         bias_rows = const.tile([P, P], BF16, name="bias_rows")
         nc.vector.memset(bias_rows[:], 0.0)
         table_probe = const.tile([P, 2], F32, name="table_probe")
         nc.vector.memset(table_probe[:], 0.0)
         nc.scalar.activation(out=table_probe[:, 1:2], in_=table_probe[:, 0:1], func=ACT.Sigmoid)
-
         idle_rows = const.tile([P, ROUND], BF16, name="idle_rows")
         nc.vector.memset(idle_rows[:], 0.0)
+        nc.vector.memset(w_scales[:].bitcast(I32), 0)
+
         for i in range(WARM_UP):
             idle_bank = product_psum.tile([P, ROUND], F32, name="idle_bank", tag="acc")
             nc.tensor.matmul(idle_bank[:], lhsT=idle_rows[:, 0:P], rhs=idle_rows[:], start=True, stop=True)
@@ -252,37 +252,41 @@ def tile_scan_pb_t_kernel(
         multiply(0, LIN_BLOCKS)
         activate(0, LIN_BLOCKS)
         quantise(1)
+        regroup(4, transpose_cat(4), on_vector=True)
         multiply(0, GATE_BLOCKS)
         activate(0, GATE_BLOCKS)
-        regroup(4, transpose_cat(4), on_vector=True)
         split_words(3)
         words_t = transpose_cat(5)
         for r in range(1, ROUNDS + 1):
             if r + LOAD_AHEAD < ROUNDS:
                 load(r + LOAD_AHEAD)
+            if r + 3 < ROUNDS:
+                split_words(r + 3)
             if r + 1 < ROUNDS:
                 regroup(2 * r + 3, words_t)
                 quantise(r + 1)
-            if r + 3 < ROUNDS:
-                split_words(r + 3)
             for c in (2 * r, 2 * r + 1):
-                if r < ROUNDS:
-                    blocks = GATE_BLOCKS if c % 2 else LIN_BLOCKS
+                blocks = GATE_BLOCKS if c % 2 else LIN_BLOCKS
+                very_last = c == HALF_ROUNDS - 1
+                if r < ROUNDS and not very_last:
                     multiply(r, blocks)
                     activate(r, blocks)
                 upd, keep = transpose_back(c - 2)
                 start_blend(c - 2, upd, keep)
+                if very_last:
+                    multiply(r, blocks)
+                    activate(r, blocks)
                 if r + 2 < ROUNDS:
                     words_t = transpose_cat(c + 4)
                     if c == 2 * r:
                         regroup(c + 4, words_t)
             end_blend(2 * r - 2)
-            if r >= LAST_WHOLE:
+            if LAST_WHOLE <= r < ROUNDS:
                 add_query(nc.gpsimd, r - 1, slice(0, 2))
             end_blend(2 * r - 1)
             if r == ROUNDS:
-                add_query(nc.vector, r - 1, slice(2, 3))
-                add_query(nc.vector, r - 1, slice(3, 4))
+                for tiles in (slice(0, 2), slice(2, 3), slice(3, 4)):
+                    add_query(nc.vector, r - 1, tiles)
             elif r >= LAST_WHOLE:
                 add_query(nc.gpsimd, r - 1, slice(2, 4))
             else:

from contextlib import ExitStack

import concourse.mybir as mybir
from concourse.masks import make_identity

F32 = mybir.dt.float32
BF16 = mybir.dt.bfloat16
I32 = mybir.dt.int32
U32 = mybir.dt.uint32
U8 = mybir.dt.uint8
FP8X4 = mybir.dt.float8_e4m3fn_x4
FP4X4 = mybir.dt.float4_e2m1fn_x4
ACT = mybir.ActivationFunctionType
ALU = mybir.AluOpType

P = 128
D = 256
K = 2 * D
TOKENS = 8 * 8 * 128
TILES = 4
ROUND = TILES * P
ROUNDS = TOKENS // ROUND
HALF = ROUND // 2
HALF_ROUNDS = 2 * ROUNDS
BLOCKS = 4
LIN_BLOCKS = (0, 1)
GATE_BLOCKS = (2, 3)
LOAD_AHEAD = 8
CAT_LEAD = 4
FIRST_SPLIT = 6
SPLIT_LEAD = CAT_LEAD + 2
LAST_WHOLE = ROUNDS - 2
BRIDGE = 64
WARM_UP = 3
SPLIT_TILES = 3
BACK_LAG = 2

FLOPS = 2 * TOKENS * K * (2 * D)


def tile_scan_pb_t_kernel(
    tc, query, wc, w_lin_words, w_lin_scales, b_lin, w_gate_words, w_gate_scales, b_gate, out
):
    nc = tc.nc

    q_rounds = query.flatten_outer_dims().rearrange("(r p j) d -> r p j d", p=P, j=TILES)
    wc_rounds = wc.flatten_outer_dims().rearrange("(r p j) d -> r p j d", p=P, j=TILES)
    out_rounds = out.flatten_outer_dims().rearrange("(r p j) d -> r p j d", p=P, j=TILES)

    with ExitStack() as stack:
        const = stack.enter_context(tc.tile_pool(name="const", bufs=1))
        cat_pool = stack.enter_context(tc.tile_pool(name="cat", bufs=ROUNDS))
        mx_pool = stack.enter_context(tc.tile_pool(name="mx", bufs=4))
        split_pool = stack.enter_context(tc.tile_pool(name="split", bufs=3))
        act_pool = stack.enter_context(tc.tile_pool(name="act", bufs=2))
        blend_pool = stack.enter_context(tc.tile_pool(name="blend", bufs=6))
        cat_t_psum = stack.enter_context(tc.psum_pool(name="cat_t_psum", bufs=1))
        product_psum = stack.enter_context(tc.psum_pool(name="product_psum", bufs=3))
        back_psum = stack.enter_context(tc.psum_pool(name="back_psum", bufs=4))
        stack.enter_context(tc.manual_schedule())

        cat = {}
        split = {}
        grouped = {}
        codes = {}
        product = {}
        pending = {}
        change = {}
        activated = {}

        def load(r, tiles=slice(0, TILES)):
            if r not in cat:
                cat[r] = cat_pool.tile([P, TILES, K], BF16, name="cat")
            nc.sync.dma_start(out=cat[r][:, tiles, 0:D], in_=q_rounds[r][:, tiles, :])
            nc.sync.dma_start(out=cat[r][:, tiles, D:K], in_=wc_rounds[r][:, tiles, :])

        def split_words(r):
            split[r] = split_pool.tile([P, 2, SPLIT_TILES, P], F32, name="split")
            nc.vector.tensor_copy(
                out=split[r][:].rearrange("p u j w -> p (j w) u"),
                in_=cat[r][:, 0:SPLIT_TILES, :].bitcast(F32).rearrange("p j (w u) -> p (j w) u", u=2),
            )

        def transpose_cat(c):
            r, half = divmod(c, 2)
            if c < FIRST_SPLIT and c % 2 == 1:
                words_t = back_psum.tile([P, 2, 2, P], F32, name="words_t", tag="bank")
            else:
                words_t = cat_t_psum.tile([P, 2, 2, P], F32, name="words_t")
            for jj in range(2):
                j = 2 * half + jj
                words = cat[r][:, j, :].bitcast(F32)
                for u in range(2):
                    apart = r in split and j < SPLIT_TILES
                    source = split[r][:, u, j, :] if apart else words[:, u : K // 2 : 2]
                    nc.tensor.transpose(words_t[:, jj, u, :], source, ident[:])
            return words_t

        def regroup(c, words_t, on_vector=False):
            r, half = divmod(c, 2)
            if half == 0:
                grouped[r] = mx_pool.tile([P, TILES, P, 4], BF16, name="grouped", align_bytes=64)
            words = grouped[r][:, 2 * half : 2 * half + 2, :, :].bitcast(F32)
            copy = nc.vector.tensor_copy if on_vector else nc.scalar.copy
            copy(out=words, in_=words_t[:].rearrange("p j u t -> p j t u"))

        def quantise(r, tiles=slice(0, TILES)):
            if r not in codes:
                code_words = mx_pool.tile([P, ROUND], U32, name="code_words", align_bytes=64)
                code_scales = mx_pool.tile([P, ROUND], U8, name="code_scales", align_bytes=64)
                codes[r] = (code_words, code_scales)
            code_words, code_scales = codes[r]
            tokens = slice(P * tiles.start, P * tiles.stop)
            nc.vector.quantize_mx(
                out=code_words[:, tokens].bitcast(FP8X4),
                scales=code_scales[:, tokens],
                in_=grouped[r][:, tiles, :, :].rearrange("p j t k -> p (j t k)"),
            )

        def bridge(columns):
            nc.tensor.matmul(columns, lhsT=idle_rows[:, 0:P], rhs=idle_rows[:, 0:BRIDGE], start=True, stop=True)

        def multiply(r, blocks):
            code_words, code_scales = codes[r]
            for b in blocks:
                acc = product_psum.tile([P, ROUND], F32, name="acc")
                if b == blocks[0]:
                    bridge(acc[:, 0:BRIDGE])
                nc.tensor.matmul_mx(
                    out=acc[:],
                    lhsT=w_words[:, 2 * P * b : 2 * P * (b + 1)].bitcast(FP4X4),
                    lhsT_scale=w_scales[:, P * b : P * (b + 1)],
                    rhs=code_words[:].bitcast(FP8X4),
                    rhs_scale=code_scales[:],
                    start=True,
                    stop=True,
                )
                product[r, b] = acc

        def activate(r, blocks):
            for b in blocks:
                activated[r, b] = act_pool.tile([P, ROUND], F32, name="act", tag="act%d" % b)
            pieces = 2 if r == ROUNDS - 1 else 1
            for i in range(pieces):
                tokens = slice(i * ROUND // pieces, (i + 1) * ROUND // pieces)
                for b in blocks:
                    is_gate = b in GATE_BLOCKS
                    nc.scalar.activation(
                        out=activated[r, b][:, tokens],
                        in_=product[r, b][:, tokens],
                        func=ACT.Sigmoid if is_gate else ACT.Tanh,
                        bias=bias_col[:, b : b + 1],
                        scale=-1.0 if is_gate else 1.0,
                    )

        def transpose_back(c):
            r, half = divmod(c, 2)
            banks = []
            for blocks in (LIN_BLOCKS, GATE_BLOCKS):
                bank = back_psum.tile([P, 2, D], F32, name="bank")
                if blocks == LIN_BLOCKS:
                    bridge(bank[:, 0, 0:BRIDGE])
                for jj in range(2):
                    tokens = slice(P * (2 * half + jj), P * (2 * half + jj + 1))
                    for i, b in enumerate(blocks):
                        nc.tensor.transpose(bank[:, jj, P * i : P * (i + 1)], activated[r, b][:, tokens], ident[:])
                banks.append(bank)
            return banks

        def start_blend(c, upd, keep):
            r, half = divmod(c, 2)
            diff = blend_pool.tile([P, 2, D], F32, name="diff")
            q = cat[r][:, 2 * half : 2 * half + 2, 0:D]
            nc.vector.tensor_tensor(out=diff[:], in0=upd[:], in1=q, op=ALU.subtract)
            pending[c] = (diff, keep)

        def end_blend(c):
            r, half = divmod(c, 2)
            if half == 0:
                change[r] = blend_pool.tile([P, TILES, D], F32, name="change")
            diff, keep = pending.pop(c)
            moved = change[r][:, 2 * half : 2 * half + 2, :]
            nc.vector.tensor_tensor(out=moved, in0=keep[:], in1=diff[:], op=ALU.mult)

        def add_query(engine, r, tiles):
            result = blend_pool.tile([P, TILES, D], F32, name="result")
            engine.tensor_tensor(
                out=result[:, tiles, :], in0=change[r][:, tiles, :], in1=cat[r][:, tiles, 0:D], op=ALU.add
            )
            nc.sync.dma_start(out=out_rounds[r][:, tiles, :], in_=result[:, tiles, :])

        ident = const.tile([P, P], F32, name="ident")
        make_identity(nc, ident[:])

        w_scales = const.tile([P, BLOCKS * P], U8, name="w_scales", align_bytes=64)
        w_words = const.tile([P, BLOCKS * 2 * P], U8, name="w_words", align_bytes=64)
        bias_rows = const.tile([P, P], BF16, name="bias_rows")
        nc.vector.memset(bias_rows[:], 0.0)
        table_probe = const.tile([P, 2], F32, name="table_probe")
        nc.vector.memset(table_probe[:], 0.0)
        nc.scalar.activation(out=table_probe[:, 1:2], in_=table_probe[:, 0:1], func=ACT.Sigmoid)
        idle_rows = const.tile([P, ROUND], BF16, name="idle_rows")
        nc.vector.memset(idle_rows[:], 0.0)
        nc.vector.memset(w_scales[:].bitcast(I32), 0)

        for i in range(WARM_UP):
            idle_bank = product_psum.tile([P, ROUND], F32, name="idle_bank", tag="acc")
            nc.tensor.matmul(idle_bank[:], lhsT=idle_rows[:, 0:P], rhs=idle_rows[:], start=True, stop=True)

        def load_weight(i, dram_words, dram_scales):
            nc.sync.dma_start(
                out=w_words[:, 2 * D * i : 2 * D * (i + 1)].bitcast(I32), in_=dram_words[0].bitcast(I32)
            )
            for quad in range(4):
                nc.sync.dma_start(
                    out=w_scales[32 * quad : 32 * quad + 4, D * i : D * (i + 1)].bitcast(I32),
                    in_=dram_scales[0, 4 * quad : 4 * quad + 4, :].bitcast(I32),
                )

        load(0, slice(0, 2))
        nc.sync.dma_start(out=bias_rows[0:2, :], in_=b_lin.rearrange("(r c) -> r c", c=P))
        nc.sync.dma_start(out=bias_rows[2:4, :], in_=b_gate.rearrange("(r c) -> r c", c=P))
        load(0, slice(2, 4))
        load(1)
        load_weight(0, w_lin_words, w_lin_scales)
        load(2)
        load_weight(1, w_gate_words, w_gate_scales)
        for r in range(3, LOAD_AHEAD + 1):
            load(r)

        bias_col = const.tile([P, BLOCKS], F32, name="bias_col")

        bias_f32 = const.tile([P, P], F32, name="bias_f32")
        nc.vector.tensor_copy(out=bias_f32[:], in_=bias_rows[:])

        def spread_biases():
            bias_t = back_psum.tile([P, P], F32, name="bias_t", tag="bank")
            nc.tensor.transpose(bias_t[:], bias_f32[:], ident[:])
            nc.vector.tensor_copy(out=bias_col[:, 0:2], in_=bias_t[:, 0:2])
            nc.vector.tensor_scalar_mul(out=bias_col[:, 2:4], in0=bias_t[:, 2:4], scalar1=-1.0)

        def live(c):
            return 0 <= c < HALF_ROUNDS

        regroup(0, transpose_cat(0))
        regroup(1, transpose_cat(1))
        spread_biases()
        quantise(0, slice(0, 2))
        quantise(0, slice(2, 4))
        regroup(2, transpose_cat(2))
        regroup(3, transpose_cat(3), on_vector=True)
        multiply(0, LIN_BLOCKS)
        activate(0, LIN_BLOCKS)
        quantise(1)
        regroup(4, transpose_cat(4), on_vector=True)
        multiply(0, GATE_BLOCKS)
        activate(0, GATE_BLOCKS)
        split_words(3)
        words_t = transpose_cat(5)
        for r in range(1, ROUNDS + 1):
            if r + LOAD_AHEAD < ROUNDS:
                load(r + LOAD_AHEAD)
            if r + 3 < ROUNDS:
                split_words(r + 3)
            if r + 1 < ROUNDS:
                regroup(2 * r + 3, words_t)
                quantise(r + 1)
            for c in (2 * r, 2 * r + 1):
                blocks = GATE_BLOCKS if c % 2 else LIN_BLOCKS
                very_last = c == HALF_ROUNDS - 1
                if r < ROUNDS and not very_last:
                    multiply(r, blocks)
                    activate(r, blocks)
                upd, keep = transpose_back(c - 2)
                start_blend(c - 2, upd, keep)
                if very_last:
                    multiply(r, blocks)
                    activate(r, blocks)
                if r + 2 < ROUNDS:
                    words_t = transpose_cat(c + 4)
                    if c == 2 * r:
                        regroup(c + 4, words_t)
            end_blend(2 * r - 2)
            if LAST_WHOLE <= r < ROUNDS:
                add_query(nc.gpsimd, r - 1, slice(0, 2))
            end_blend(2 * r - 1)
            if r == ROUNDS:
                for tiles in (slice(0, 2), slice(2, 3), slice(3, 4)):
                    add_query(nc.vector, r - 1, tiles)
            elif r >= LAST_WHOLE:
                add_query(nc.gpsimd, r - 1, slice(2, 4))
            else:
                add_query(nc.gpsimd, r - 1, slice(0, TILES))
